import numpy as np
import ml_dtypes


def mxq(x, axis, fmt="e4m3"):
    dtype, down = {"e4m3": (ml_dtypes.float8_e4m3fn, 7), "e5m2": (ml_dtypes.float8_e5m2, 14)}[fmt]
    v = np.moveaxis(np.asarray(x, np.float32).astype(ml_dtypes.bfloat16).astype(np.float64), axis, -1)
    blocks = v.reshape(v.shape[:-1] + (-1, 32))
    amax = np.abs(blocks).max(-1, keepdims=True)
    byte = np.maximum(np.where(amax > 0, np.frexp(amax)[1] - 1 + 127, 0) - down, 1)
    scale = np.exp2(byte - 127.0)
    codes = (blocks / scale).astype(np.float32).astype(dtype).astype(np.float64)
    return np.moveaxis((codes * scale).reshape(v.shape), -1, axis)


WIDE = False


def mx_kscale(k):
    if not WIDE:
        return np.ones(k)
    levels = np.array([10, -10, 5, -5, 0])
    a = np.random.permutation(np.resize(levels, k // 512 * 4)).reshape(k // 512, 4)
    idx = np.arange(k)
    return np.exp2(a[idx // 512, idx % 128 // 32])


BF16 = ml_dtypes.bfloat16


def bf(x):
    return np.asarray(x, np.float32).astype(BF16)


def f64(x):
    return np.asarray(x).astype(np.float64)


E2M1 = np.array([0.0, 0.5, 1.0, 1.5, 2.0, 3.0, 4.0, 6.0, -0.0, -0.5, -1.0, -1.5, -2.0, -3.0, -4.0, -6.0])


def pack_weight(w, fmt):
    k, n = w.shape
    w = f64(bf(w)).reshape(k // 32, 32, n)
    amax = np.abs(w).max(1)
    if fmt == "e4m3":
        byte = np.frexp(amax)[1] - 1 + 127 - 7
    else:
        mant, ex = np.frexp(amax / 6.0)
        byte = np.where(mant > 0.5, ex, ex - 1) + 127
    byte = np.clip(np.where(amax > 0, byte, 1), 1, 254)
    scaled = (w * np.exp2(127.0 - byte)[:, None, :]).reshape(k, n).astype(np.float32)
    by_word = np.ascontiguousarray(scaled.reshape(k // 512, 128, 4, n).transpose(0, 1, 3, 2))
    if fmt == "e4m3":
        words = by_word.astype(ml_dtypes.float8_e4m3fn).view(np.uint8)
    else:
        c = by_word.astype(ml_dtypes.float4_e2m1fn).view(np.uint8) & 0xF
        words = c[..., 0::2] | (c[..., 1::2] << 4)
    return np.ascontiguousarray(words), np.ascontiguousarray(byte.astype(np.uint8).reshape(k // 512, 16, n))


def unpack_weight(words, scales, fmt):
    g, p, n, _ = words.shape
    if fmt == "e4m3":
        vals = np.ascontiguousarray(words).view(ml_dtypes.float8_e4m3fn).astype(np.float64)
    else:
        nib = np.empty((g, p, n, 4), np.uint8)
        nib[..., 0::2] = words & 0xF
        nib[..., 1::2] = words >> 4
        vals = E2M1[nib]
    vals = vals * np.repeat(np.exp2(scales.astype(np.float64) - 127.0), 8, axis=1)[..., None]
    return vals.transpose(0, 1, 3, 2).reshape(g * 512, n)


B, D, U = 4096, 256, 256
KD = 3 * U + D
FMT = "e4m3"


def setup_inputs():
    s = np.ones(KD)
    s[3 * U:] = np.sort(mx_kscale(KD))[::KD // D]

    def gate():
        return pack_weight(np.random.standard_normal((KD, U)) * 1.25 / np.sqrt(KD) / s[:, None], FMT)

    def bias():
        return bf(np.random.standard_normal(U) * 0.5)

    x = bf(np.random.standard_normal((B, D)) * s[3 * U:])
    left_state = bf(np.random.standard_normal((B, U)))
    top_state = bf(np.random.standard_normal((B, U)))
    diagonal_state = bf(np.random.standard_normal((B, U)))
    h_cand = bf(np.tanh(np.random.standard_normal((B, U))))
    w_zi_words, w_zi_scales = gate()
    b_zi = bias()
    w_zl_words, w_zl_scales = gate()
    b_zl = bias()
    w_zt_words, w_zt_scales = gate()
    b_zt = bias()
    w_zd_words, w_zd_scales = gate()
    b_zd = bias()
    return {"x": x,
            "left_state": left_state,
            "top_state": top_state,
            "diagonal_state": diagonal_state,
            "h_cand": h_cand,
            "w_zi_words": w_zi_words, "w_zi_scales": w_zi_scales, "b_zi": b_zi,
            "w_zl_words": w_zl_words, "w_zl_scales": w_zl_scales, "b_zl": b_zl,
            "w_zt_words": w_zt_words, "w_zt_scales": w_zt_scales, "b_zt": b_zt,
            "w_zd_words": w_zd_words, "w_zd_scales": w_zd_scales, "b_zd": b_zd}


def reference(x, left_state, top_state, diagonal_state, h_cand, w_zi_words, w_zi_scales, b_zi, w_zl_words, w_zl_scales, b_zl, w_zt_words, w_zt_scales, b_zt, w_zd_words, w_zd_scales, b_zd):
    left, top, diag = f64(left_state), f64(top_state), f64(diagonal_state)
    q = np.concatenate([left, top, diag, f64(x)], axis=1)
    W = np.concatenate([unpack_weight(w_zi_words, w_zi_scales, FMT), unpack_weight(w_zl_words, w_zl_scales, FMT),
                        unpack_weight(w_zt_words, w_zt_scales, FMT), unpack_weight(w_zd_words, w_zd_scales, FMT)], axis=1)
    b = np.concatenate([f64(b_zi), f64(b_zl), f64(b_zt), f64(b_zd)])
    g = ((mxq(q, 1, "e4m3") @ W) + b).reshape(-1, 4, U)
    e = np.exp(g - g.max(axis=1, keepdims=True))
    z = e / e.sum(axis=1, keepdims=True)
    return z[:, 1] * left + z[:, 2] * top + z[:, 3] * diag + z[:, 0] * f64(h_cand)

@@ -1,0 +1,319 @@
+from contextlib import ExitStack
+
+import concourse.mybir as mybir
+from concourse.masks import make_identity
+
+FLOPS = 2 * 4096 * 1024 * 1024
+
+F32 = mybir.dt.float32
+BF16 = mybir.dt.bfloat16
+I32 = mybir.dt.int32
+U32 = mybir.dt.uint32
+U8 = mybir.dt.uint8
+FP8X4 = mybir.dt.float8_e4m3fn_x4
+ALU = mybir.AluOpType
+ACT = mybir.ActivationFunctionType
+
+P = 128
+ROWS = 4096
+UNITS = 256
+K = 1024
+GATES = 4
+K_PASS = 512
+PASSES = K // K_PASS
+WORDS = K_PASS // 2
+
+ROWS_PER_PARTITION = ROWS // P
+TILES = 4
+COLS = TILES * P
+BLOCKS = ROWS_PER_PARTITION // TILES
+HALVES = UNITS // P
+STAGES = BLOCKS * HALVES
+BATCH = 4
+DELAY = 2
+
+
+def tile_multidimensinalgrucell_pb_t_kernel(
+    tc,
+    x,
+    left_state,
+    top_state,
+    diagonal_state,
+    h_cand,
+    w_zi_words,
+    w_zi_scales,
+    b_zi,
+    w_zl_words,
+    w_zl_scales,
+    b_zl,
+    w_zt_words,
+    w_zt_scales,
+    b_zt,
+    w_zd_words,
+    w_zd_scales,
+    b_zd,
+    out,
+):
+    nc = tc.nc
+    gate_words = (w_zi_words, w_zl_words, w_zt_words, w_zd_words)
+    gate_scales = (w_zi_scales, w_zl_scales, w_zt_scales, w_zd_scales)
+    gate_bias = (b_zi, b_zl, b_zt, b_zd)
+    q_parts = (left_state, top_state, diagonal_state, x)
+
+    def by_partition(rows):
+        return rows.rearrange("(p t) c -> p t c", t=ROWS_PER_PARTITION)
+
+    with ExitStack() as ctx:
+        ctx.enter_context(tc.manual_schedule())
+        keep = ctx.enter_context(tc.tile_pool(name="keep", bufs=1))
+        rows_pool = ctx.enter_context(tc.tile_pool(name="rows", bufs=3))
+        quant = ctx.enter_context(tc.tile_pool(name="quant", bufs=2))
+        work = ctx.enter_context(tc.tile_pool(name="work", bufs=2))
+        gate_psum = ctx.enter_context(tc.psum_pool(name="gate_psum", bufs=1))
+        state_psum = ctx.enter_context(tc.psum_pool(name="state_psum", bufs=1))
+        turn_psum = ctx.enter_context(tc.psum_pool(name="turn_psum", bufs=2))
+
+        w_codes = keep.tile([P, GATES, PASSES, UNITS], U32, align_bytes=64)
+        w_planes = keep.tile([P, GATES, PASSES, UNITS], U8, align_bytes=64)
+        bias_rows = keep.tile([P, P], BF16)
+        bias = keep.tile([P, GATES * HALVES], F32)
+        ident_bf16 = keep.tile([P, P], BF16)
+        ident_f32 = keep.tile([P, P], F32)
+
+        nc.vector.memset(w_planes[:].bitcast(I32), 0)
+        nc.vector.memset(bias_rows[:].bitcast(I32), 0)
+        make_identity(nc, ident_f32[:])
+        make_identity(nc, ident_bf16[:])
+
+        q_rows = {}
+        h_rows = {}
+
+        def load_rows(b):
+            tiles = slice(b * TILES, (b + 1) * TILES)
+            q_rows[b] = rows_pool.tile([P, TILES, K], BF16, name="q_rows")
+            h_rows[b] = rows_pool.tile([P, TILES, UNITS], BF16, name="h_rows")
+            for part, rows in enumerate(q_parts):
+                nc.sync.dma_start(
+                    out=q_rows[b][:, :, part * UNITS : (part + 1) * UNITS],
+                    in_=by_partition(rows)[:, tiles, :],
+                )
+            nc.sync.dma_start(out=h_rows[b][:], in_=by_partition(h_cand)[:, tiles, :])
+
+        load_rows(0)
+        for j in range(GATES):
+            nc.sync.dma_start(
+                out=w_codes[:, j, :, :].bitcast(I32),
+                in_=gate_words[j].rearrange("g p n t -> p g (n t)").bitcast(I32),
+            )
+        for j in range(GATES):
+            scale_rows = gate_scales[j].rearrange("g q n -> q g n")
+            for quadrant in range(4):
+                nc.sync.dma_start(
+                    out=w_planes[32 * quadrant : 32 * quadrant + 4, j, :, :].bitcast(I32),
+                    in_=scale_rows[4 * quadrant : 4 * quadrant + 4, :, :].bitcast(I32),
+                )
+            nc.scalar.dma_start(
+                out=bias_rows[HALVES * j : HALVES * (j + 1), :],
+                in_=gate_bias[j].rearrange("(h u) -> h u", h=HALVES),
+            )
+        load_rows(1)
+
+        bias_turned = turn_psum.tile([P, P], BF16, tag="turn")
+        nc.tensor.transpose(bias_turned[:], bias_rows[:], ident_bf16[:])
+        nc.vector.tensor_copy(out=bias[:], in_=bias_turned[:, 0 : GATES * HALVES])
+
+        grouped = {}
+        q_codes = {}
+        q_planes = {}
+        acc = {}
+        turned_states = {}
+        top_gate = {}
+        weights = {}
+        weighted = {}
+        sums = {}
+
+        def transpose_q(b):
+            grouped[b] = quant.tile([P, PASSES, 4 * COLS], BF16, name="grouped", align_bytes=64)
+            for g in range(PASSES):
+                for pair in range(TILES // 2):
+                    turned = turn_psum.tile([P, 2, 2 * P], F32, name="turned", tag="turn")
+                    for i in range(2):
+                        words = q_rows[b][:, 2 * pair + i, :].bitcast(F32)
+                        for u in range(2):
+                            nc.tensor.transpose(
+                                turned[:, u, i * P : (i + 1) * P],
+                                words[:, WORDS * g + u : WORDS * (g + 1) : 2],
+                                ident_f32[:],
+                            )
+                    side_by_side = grouped[b][:, g, pair * 8 * P : (pair + 1) * 8 * P].bitcast(F32)
+                    nc.scalar.copy(
+                        out=side_by_side.rearrange("p (c u) -> p c u", u=2),
+                        in_=turned[:].rearrange("p u c -> p c u"),
+                    )
+
+        def quantise_q(b):
+            q_codes[b] = quant.tile([P, PASSES, COLS], U32, name="q_codes", align_bytes=64)
+            q_planes[b] = quant.tile([P, PASSES, COLS], U8, name="q_planes", align_bytes=64)
+            for g in range(PASSES):
+                nc.vector.quantize_mx(
+                    out=q_codes[b][:, g, :].bitcast(FP8X4),
+                    scales=q_planes[b][:, g, :],
+                    in_=grouped[b][:, g, :],
+                )
+
+        def multiply(s):
+            b, h = divmod(s, HALVES)
+            units = slice(h * P, (h + 1) * P)
+            acc[s] = []
+            for j in range(GATES):
+                bank = gate_psum.tile([P, COLS], F32, name="acc%d" % j)
+                for g in range(PASSES):
+                    nc.tensor.matmul_mx(
+                        out=bank[:],
+                        lhsT=w_codes[:, j, g, units].bitcast(FP8X4),
+                        lhsT_scale=w_planes[:, j, g, units],
+                        rhs=q_codes[b][:, g, :].bitcast(FP8X4),
+                        rhs_scale=q_planes[b][:, g, :],
+                        start=(g == 0),
+                        stop=(g == PASSES - 1),
+                    )
+                acc[s].append(bank)
+
+        def bias_of(s, j):
+            column = HALVES * j + s % HALVES
+            return bias[:, column : column + 1]
+
+        def start_maximum(s):
+            top_gate[s] = work.tile([P, COLS], F32, name="top_gate")
+            nc.scalar.activation(
+                out=top_gate[s][:], in_=acc[s][0][:], func=ACT.Identity, bias=bias_of(s, 0), scale=1.0
+            )
+
+        def transpose_states(s):
+            b, h = divmod(s, HALVES)
+            turned_states[s] = []
+            for j in range(GATES):
+                if j % 2 == 0:
+                    bank = state_psum.tile([P, 2, COLS], BF16, name="states%d" % (j // 2))
+                for t in range(TILES):
+                    if j == 0:
+                        rows = h_rows[b][:, t, h * P : (h + 1) * P]
+                    else:
+                        first = (j - 1) * UNITS + h * P
+                        rows = q_rows[b][:, t, first : first + P]
+                    nc.tensor.transpose(bank[:, j % 2, t * P : (t + 1) * P], rows, ident_bf16[:])
+                turned_states[s].append(bank[:, j % 2, :])
+
+        def exponentials(s):
+            for j in range(1, GATES):
+                nc.vector.scalar_tensor_tensor(
+                    out=top_gate[s][:],
+                    in0=acc[s][j][:],
+                    scalar=bias_of(s, j),
+                    in1=top_gate[s][:],
+                    op0=ALU.add,
+                    op1=ALU.max,
+                )
+            weights[s] = work.tile([P, GATES, COLS], F32, name="weights")
+            for j in range(GATES):
+                nc.vector.scalar_tensor_tensor(
+                    out=weights[s][:, j, :],
+                    in0=acc[s][j][:],
+                    scalar=bias_of(s, j),
+                    in1=top_gate[s][:],
+                    op0=ALU.add,
+                    op1=ALU.subtract,
+                )
+                nc.scalar.activation(out=weights[s][:, j, :], in_=weights[s][:, j, :], func=ACT.Exp)
+
+        def add_gates(terms, total):
+            halves = work.tile([P, 2, COLS], F32, name="halves")
+            nc.gpsimd.tensor_tensor(
+                out=halves[:], in0=terms[:, 0:2, :], in1=terms[:, 2:4, :], op=ALU.add
+            )
+            nc.gpsimd.tensor_tensor(out=total, in0=halves[:, 0, :], in1=halves[:, 1, :], op=ALU.add)
+
+        def sum_weights(s):
+            n, i = divmod(s, BATCH)
+            if i == 0:
+                sums[n] = work.tile([P, 2, BATCH, COLS], F32, name="sums")
+            add_gates(weights[s], sums[n][:, 0, i, :])
+
+        def weigh_states(s):
+            n, i = divmod(s, BATCH)
+            weighted[s] = work.tile([P, GATES, COLS], F32, name="weighted")
+            for j in range(GATES):
+                nc.vector.tensor_tensor(
+                    out=weighted[s][:, j, :],
+                    in0=weights[s][:, j, :],
+                    in1=turned_states[s][j],
+                    op=ALU.mult,
+                )
+            add_gates(weighted[s], sums[n][:, 1, i, :])
+
+        def logarithms(n):
+            for i in range(BATCH):
+                nc.scalar.activation(out=sums[n][:, 0, i, :], in_=sums[n][:, 0, i, :], func=ACT.Ln)
+
+        def reciprocals(n):
+            for i in range(BATCH):
+                nc.scalar.activation(
+                    out=sums[n][:, 0, i, :], in_=sums[n][:, 0, i, :], func=ACT.Exp, scale=-1.0
+                )
+
+        def normalise(n):
+            for i in range(BATCH):
+                nc.vector.tensor_tensor(
+                    out=sums[n][:, 1, i, :], in0=sums[n][:, 1, i, :], in1=sums[n][:, 0, i, :], op=ALU.mult
+                )
+
+        def store(n):
+            for i in range(BATCH):
+                b, h = divmod(n * BATCH + i, HALVES)
+                if h == 0:
+                    out_rows = work.tile([P, TILES, UNITS], F32, name="out_rows")
+                back = turn_psum.tile([P, TILES, P], F32, name="back", tag="turn")
+                for t in range(TILES):
+                    nc.tensor.transpose(
+                        back[:, t, :], sums[n][:, 1, i, t * P : (t + 1) * P], ident_f32[:]
+                    )
+                nc.scalar.copy(out=out_rows[:, :, h * P : (h + 1) * P], in_=back[:])
+                if h == HALVES - 1:
+                    nc.sync.dma_start(
+                        out=by_partition(out)[:, b * TILES : (b + 1) * TILES, :], in_=out_rows[:]
+                    )
+
+        transpose_q(0)
+        quantise_q(0)
+        multiply(0)
+        start_maximum(0)
+        transpose_states(0)
+
+        first_inversion = BATCH - 1 + DELAY
+        for s in range(STAGES + DELAY + 2):
+            b, h = divmod(s, HALVES)
+            n, step = divmod(s - first_inversion, BATCH)
+            if s < STAGES and h == 1 and b + 1 < BLOCKS:
+                quantise_q(b + 1)
+            if n >= 0 and step == 2:
+                normalise(n)
+            if s < STAGES:
+                exponentials(s)
+                sum_weights(s)
+            if s + 1 < STAGES:
+                multiply(s + 1)
+                start_maximum(s + 1)
+            if h == 0 and b + 1 < BLOCKS:
+                transpose_q(b + 1)
+                if b + 2 < BLOCKS:
+                    load_rows(b + 2)
+            if n >= 0 and step == 0:
+                logarithms(n)
+            if n >= 0 and step == 1:
+                reciprocals(n)
+            if n >= 0 and step == 2:
+                store(n)
+            if s < STAGES:
+                weigh_states(s)
+            if s + 1 < STAGES:
+                transpose_states(s + 1)

@@ -29,8 +29,13 @@ COLS = TILES * P
 BLOCKS = ROWS_PER_PARTITION // TILES
 HALVES = UNITS // P
 STAGES = BLOCKS * HALVES
+CHUNKS = BLOCKS * PASSES
 BATCH = 4
-DELAY = 2
+
+TURN_AHEAD = 4
+QUANTISE_AHEAD = 2
+LOAD_AHEAD = 3
+LN_BEHIND = 1
 
 
 def tile_multidimensinalgrucell_pb_t_kernel(
@@ -66,9 +71,11 @@ def tile_multidimensinalgrucell_pb_t_kernel(
     with ExitStack() as ctx:
         ctx.enter_context(tc.manual_schedule())
         keep = ctx.enter_context(tc.tile_pool(name="keep", bufs=1))
-        rows_pool = ctx.enter_context(tc.tile_pool(name="rows", bufs=3))
-        quant = ctx.enter_context(tc.tile_pool(name="quant", bufs=2))
-        work = ctx.enter_context(tc.tile_pool(name="work", bufs=2))
+        rows_pool = ctx.enter_context(tc.tile_pool(name="rows", bufs=LOAD_AHEAD + 1))
+        grouped_pool = ctx.enter_context(tc.tile_pool(name="grouped", bufs=TURN_AHEAD))
+        pairs = ctx.enter_context(tc.tile_pool(name="pairs", bufs=2))
+        weights_pool = ctx.enter_context(tc.tile_pool(name="weights", bufs=3))
+        sums_pool = ctx.enter_context(tc.tile_pool(name="sums", bufs=2 * BATCH))
         gate_psum = ctx.enter_context(tc.psum_pool(name="gate_psum", bufs=1))
         state_psum = ctx.enter_context(tc.psum_pool(name="state_psum", bufs=1))
         turn_psum = ctx.enter_context(tc.psum_pool(name="turn_psum", bufs=2))
@@ -116,11 +123,16 @@ def tile_multidimensinalgrucell_pb_t_kernel(
                 out=bias_rows[HALVES * j : HALVES * (j + 1), :],
                 in_=gate_bias[j].rearrange("(h u) -> h u", h=HALVES),
             )
-        load_rows(1)
+        for b in range(1, LOAD_AHEAD):
+            load_rows(b)
 
         bias_turned = turn_psum.tile([P, P], BF16, tag="turn")
         nc.tensor.transpose(bias_turned[:], bias_rows[:], ident_bf16[:])
         nc.vector.tensor_copy(out=bias[:], in_=bias_turned[:, 0 : GATES * HALVES])
+
+        def bias_of(s, j):
+            column = HALVES * j + s % HALVES
+            return bias[:, column : column + 1]
 
         grouped = {}
         q_codes = {}
@@ -132,66 +144,87 @@ def tile_multidimensinalgrucell_pb_t_kernel(
         weighted = {}
         sums = {}
 
-        def transpose_q(b):
-            grouped[b] = quant.tile([P, PASSES, 4 * COLS], BF16, name="grouped", align_bytes=64)
-            for g in range(PASSES):
-                for pair in range(TILES // 2):
-                    turned = turn_psum.tile([P, 2, 2 * P], F32, name="turned", tag="turn")
-                    for i in range(2):
-                        words = q_rows[b][:, 2 * pair + i, :].bitcast(F32)
-                        for u in range(2):
-                            nc.tensor.transpose(
-                                turned[:, u, i * P : (i + 1) * P],
-                                words[:, WORDS * g + u : WORDS * (g + 1) : 2],
-                                ident_f32[:],
-                            )
-                    side_by_side = grouped[b][:, g, pair * 8 * P : (pair + 1) * 8 * P].bitcast(F32)
-                    nc.scalar.copy(
-                        out=side_by_side.rearrange("p (c u) -> p c u", u=2),
-                        in_=turned[:].rearrange("p u c -> p c u"),
-                    )
-
-        def quantise_q(b):
-            q_codes[b] = quant.tile([P, PASSES, COLS], U32, name="q_codes", align_bytes=64)
-            q_planes[b] = quant.tile([P, PASSES, COLS], U8, name="q_planes", align_bytes=64)
-            for g in range(PASSES):
-                nc.vector.quantize_mx(
-                    out=q_codes[b][:, g, :].bitcast(FP8X4),
-                    scales=q_planes[b][:, g, :],
-                    in_=grouped[b][:, g, :],
+        def transpose_q(c):
+            b, g = divmod(c, PASSES)
+            grouped[c] = grouped_pool.tile([P, 4 * COLS], BF16, name="grouped", align_bytes=64)
+            banks = []
+            for pair in range(TILES // 2):
+                turned = turn_psum.tile([P, 2, 2 * P], F32, name="turned", tag="turn")
+                for i in range(2):
+                    words = q_rows[b][:, 2 * pair + i, :].bitcast(F32)
+                    for u in range(2):
+                        nc.tensor.transpose(
+                            turned[:, u, i * P : (i + 1) * P],
+                            words[:, WORDS * g + u : WORDS * (g + 1) : 2],
+                            ident_f32[:],
+                        )
+                banks.append(turned)
+            for pair in range(TILES // 2):
+                side_by_side = grouped[c][:, pair * 8 * P : (pair + 1) * 8 * P].bitcast(F32)
+                nc.scalar.copy(
+                    out=side_by_side.rearrange("p (c u) -> p c u", u=2),
+                    in_=banks[pair][:].rearrange("p u c -> p c u"),
                 )
 
-        def multiply(s):
+        def quantise_q(c):
+            b, g = divmod(c, PASSES)
+            if g == 0:
+                q_codes[b] = pairs.tile([P, PASSES, COLS], U32, name="q_codes", align_bytes=64)
+                q_planes[b] = pairs.tile([P, PASSES, COLS], U8, name="q_planes", align_bytes=64)
+            nc.vector.quantize_mx(
+                out=q_codes[b][:, g, :].bitcast(FP8X4),
+                scales=q_planes[b][:, g, :],
+                in_=grouped[c][:],
+            )
+
+        def multiply(s, j):
             b, h = divmod(s, HALVES)
             units = slice(h * P, (h + 1) * P)
-            acc[s] = []
-            for j in range(GATES):
-                bank = gate_psum.tile([P, COLS], F32, name="acc%d" % j)
-                for g in range(PASSES):
-                    nc.tensor.matmul_mx(
-                        out=bank[:],
-                        lhsT=w_codes[:, j, g, units].bitcast(FP8X4),
-                        lhsT_scale=w_planes[:, j, g, units],
-                        rhs=q_codes[b][:, g, :].bitcast(FP8X4),
-                        rhs_scale=q_planes[b][:, g, :],
-                        start=(g == 0),
-                        stop=(g == PASSES - 1),
-                    )
-                acc[s].append(bank)
+            acc[s, j] = gate_psum.tile([P, COLS], F32, name="acc%d" % j)
+            for g in range(PASSES):
+                nc.tensor.matmul_mx(
+                    out=acc[s, j][:],
+                    lhsT=w_codes[:, j, g, units].bitcast(FP8X4),
+                    lhsT_scale=w_planes[:, j, g, units],
+                    rhs=q_codes[b][:, g, :].bitcast(FP8X4),
+                    rhs_scale=q_planes[b][:, g, :],
+                    start=(g == 0),
+                    stop=(g == PASSES - 1),
+                )
 
-        def bias_of(s, j):
-            column = HALVES * j + s % HALVES
-            return bias[:, column : column + 1]
-
-        def start_maximum(s):
-            top_gate[s] = work.tile([P, COLS], F32, name="top_gate")
+        def first_gate(s):
+            top_gate[s] = pairs.tile([P, COLS], F32, name="top_gate")
             nc.scalar.activation(
-                out=top_gate[s][:], in_=acc[s][0][:], func=ACT.Identity, bias=bias_of(s, 0), scale=1.0
+                out=top_gate[s][:], in_=acc[s, 0][:], func=ACT.Identity, bias=bias_of(s, 0), scale=1.0
             )
+
+        def larger_gate(s, j):
+            nc.vector.scalar_tensor_tensor(
+                out=top_gate[s][:],
+                in0=acc[s, j][:],
+                scalar=bias_of(s, j),
+                in1=top_gate[s][:],
+                op0=ALU.add,
+                op1=ALU.max,
+            )
+
+        def below_top(s, j):
+            if j == 0:
+                weights[s] = weights_pool.tile([P, GATES, COLS], F32, name="weights")
+            nc.vector.scalar_tensor_tensor(
+                out=weights[s][:, j, :],
+                in0=acc[s, j][:],
+                scalar=bias_of(s, j),
+                in1=top_gate[s][:],
+                op0=ALU.add,
+                op1=ALU.subtract,
+            )
+
+        def exponential(s, j):
+            nc.scalar.activation(out=weights[s][:, j, :], in_=weights[s][:, j, :], func=ACT.Exp)
 
         def transpose_states(s):
             b, h = divmod(s, HALVES)
-            turned_states[s] = []
             for j in range(GATES):
                 if j % 2 == 0:
                     bank = state_psum.tile([P, 2, COLS], BF16, name="states%d" % (j // 2))
@@ -202,118 +235,99 @@ def tile_multidimensinalgrucell_pb_t_kernel(
                         first = (j - 1) * UNITS + h * P
                         rows = q_rows[b][:, t, first : first + P]
                     nc.tensor.transpose(bank[:, j % 2, t * P : (t + 1) * P], rows, ident_bf16[:])
-                turned_states[s].append(bank[:, j % 2, :])
-
-        def exponentials(s):
-            for j in range(1, GATES):
-                nc.vector.scalar_tensor_tensor(
-                    out=top_gate[s][:],
-                    in0=acc[s][j][:],
-                    scalar=bias_of(s, j),
-                    in1=top_gate[s][:],
-                    op0=ALU.add,
-                    op1=ALU.max,
-                )
-            weights[s] = work.tile([P, GATES, COLS], F32, name="weights")
-            for j in range(GATES):
-                nc.vector.scalar_tensor_tensor(
-                    out=weights[s][:, j, :],
-                    in0=acc[s][j][:],
-                    scalar=bias_of(s, j),
-                    in1=top_gate[s][:],
-                    op0=ALU.add,
-                    op1=ALU.subtract,
-                )
-                nc.scalar.activation(out=weights[s][:, j, :], in_=weights[s][:, j, :], func=ACT.Exp)
+                turned_states[s, j] = bank[:, j % 2, :]
 
         def add_gates(terms, total):
-            halves = work.tile([P, 2, COLS], F32, name="halves")
+            halves = pairs.tile([P, 2, COLS], F32, name="halves")
             nc.gpsimd.tensor_tensor(
                 out=halves[:], in0=terms[:, 0:2, :], in1=terms[:, 2:4, :], op=ALU.add
             )
             nc.gpsimd.tensor_tensor(out=total, in0=halves[:, 0, :], in1=halves[:, 1, :], op=ALU.add)
 
         def sum_weights(s):
-            n, i = divmod(s, BATCH)
-            if i == 0:
-                sums[n] = work.tile([P, 2, BATCH, COLS], F32, name="sums")
-            add_gates(weights[s], sums[n][:, 0, i, :])
+            sums[s] = sums_pool.tile([P, 2, COLS], F32, name="sums")
+            add_gates(weights[s], sums[s][:, 0, :])
 
         def weigh_states(s):
-            n, i = divmod(s, BATCH)
-            weighted[s] = work.tile([P, GATES, COLS], F32, name="weighted")
+            weighted[s] = pairs.tile([P, GATES, COLS], F32, name="weighted")
             for j in range(GATES):
                 nc.vector.tensor_tensor(
                     out=weighted[s][:, j, :],
                     in0=weights[s][:, j, :],
-                    in1=turned_states[s][j],
+                    in1=turned_states[s, j],
                     op=ALU.mult,
                 )
-            add_gates(weighted[s], sums[n][:, 1, i, :])
+            add_gates(weighted[s], sums[s][:, 1, :])
 
-        def logarithms(n):
-            for i in range(BATCH):
-                nc.scalar.activation(out=sums[n][:, 0, i, :], in_=sums[n][:, 0, i, :], func=ACT.Ln)
+        def logarithm(s):
+            nc.scalar.activation(out=sums[s][:, 0, :], in_=sums[s][:, 0, :], func=ACT.Ln)
 
-        def reciprocals(n):
-            for i in range(BATCH):
-                nc.scalar.activation(
-                    out=sums[n][:, 0, i, :], in_=sums[n][:, 0, i, :], func=ACT.Exp, scale=-1.0
-                )
+        def reciprocal(s):
+            nc.scalar.activation(out=sums[s][:, 0, :], in_=sums[s][:, 0, :], func=ACT.Exp, scale=-1.0)
 
-        def normalise(n):
-            for i in range(BATCH):
-                nc.vector.tensor_tensor(
-                    out=sums[n][:, 1, i, :], in0=sums[n][:, 1, i, :], in1=sums[n][:, 0, i, :], op=ALU.mult
-                )
+        def normalise(s):
+            nc.vector.tensor_tensor(
+                out=sums[s][:, 1, :], in0=sums[s][:, 1, :], in1=sums[s][:, 0, :], op=ALU.mult
+            )
 
-        def store(n):
-            for i in range(BATCH):
-                b, h = divmod(n * BATCH + i, HALVES)
-                if h == 0:
-                    out_rows = work.tile([P, TILES, UNITS], F32, name="out_rows")
+        def store(b):
+            out_rows = pairs.tile([P, TILES, UNITS], F32, name="out_rows")
+            for h in range(HALVES):
                 back = turn_psum.tile([P, TILES, P], F32, name="back", tag="turn")
                 for t in range(TILES):
                     nc.tensor.transpose(
-                        back[:, t, :], sums[n][:, 1, i, t * P : (t + 1) * P], ident_f32[:]
+                        back[:, t, :], sums[b * HALVES + h][:, 1, t * P : (t + 1) * P], ident_f32[:]
                     )
                 nc.scalar.copy(out=out_rows[:, :, h * P : (h + 1) * P], in_=back[:])
-                if h == HALVES - 1:
-                    nc.sync.dma_start(
-                        out=by_partition(out)[:, b * TILES : (b + 1) * TILES, :], in_=out_rows[:]
-                    )
+            nc.sync.dma_start(out=by_partition(out)[:, b * TILES : (b + 1) * TILES, :], in_=out_rows[:])
 
-        transpose_q(0)
-        quantise_q(0)
-        multiply(0)
-        start_maximum(0)
-        transpose_states(0)
+        for c in range(QUANTISE_AHEAD):
+            transpose_q(c)
+            quantise_q(c)
+        for j in range(GATES):
+            multiply(0, j)
+        first_gate(0)
+        for c in range(QUANTISE_AHEAD, TURN_AHEAD):
+            transpose_q(c)
+        for j in range(1, GATES):
+            larger_gate(0, j)
 
-        first_inversion = BATCH - 1 + DELAY
-        for s in range(STAGES + DELAY + 2):
-            b, h = divmod(s, HALVES)
-            n, step = divmod(s - first_inversion, BATCH)
-            if s < STAGES and h == 1 and b + 1 < BLOCKS:
-                quantise_q(b + 1)
-            if n >= 0 and step == 2:
-                normalise(n)
+        first_ln = BATCH - 1 + LN_BEHIND
+        for s in range(STAGES + LN_BEHIND + 3):
+            n, step = divmod(s - first_ln, BATCH)
+            finishing = 0 <= n
+            if s + QUANTISE_AHEAD < CHUNKS:
+                quantise_q(s + QUANTISE_AHEAD)
+            for j in range(GATES):
+                if s < STAGES:
+                    below_top(s, j)
+                if s + 1 < STAGES:
+                    multiply(s + 1, j)
+                    if j == 0:
+                        first_gate(s + 1)
             if s < STAGES:
-                exponentials(s)
+                for j in range(GATES):
+                    exponential(s, j)
                 sum_weights(s)
+            if 1 <= s <= STAGES:
+                weigh_states(s - 1)
+            if finishing and step >= 2:
+                for h in range(HALVES):
+                    normalise(n * BATCH + (step - 2) * HALVES + h)
             if s + 1 < STAGES:
-                multiply(s + 1)
-                start_maximum(s + 1)
-            if h == 0 and b + 1 < BLOCKS:
-                transpose_q(b + 1)
-                if b + 2 < BLOCKS:
-                    load_rows(b + 2)
-            if n >= 0 and step == 0:
-                logarithms(n)
-            if n >= 0 and step == 1:
-                reciprocals(n)
-            if n >= 0 and step == 2:
-                store(n)
+                for j in range(1, GATES):
+                    larger_gate(s + 1, j)
+            if s + TURN_AHEAD < CHUNKS:
+                transpose_q(s + TURN_AHEAD)
+            if finishing and step >= 2:
+                store(n * (BATCH // HALVES) + step - 2)
             if s < STAGES:
-                weigh_states(s)
-            if s + 1 < STAGES:
-                transpose_states(s + 1)
+                transpose_states(s)
+            if finishing and 1 <= step <= 2:
+                for h in range(HALVES):
+                    reciprocal(n * BATCH + (step - 1) * HALVES + h)
+            if finishing and step == 0:
+                for i in range(BATCH):
+                    logarithm(n * BATCH + i)
+            if s % HALVES == 1 and s // HALVES + LOAD_AHEAD < BLOCKS:
+                load_rows(s // HALVES + LOAD_AHEAD)

@@ -234,7 +234,13 @@ def tile_multidimensinalgrucell_pb_t_kernel(
                     else:
                         first = (j - 1) * UNITS + h * P
                         rows = q_rows[b][:, t, first : first + P]
-                    nc.tensor.transpose(bank[:, j % 2, t * P : (t + 1) * P], rows, ident_bf16[:])
+                    turned = bank[:, j % 2, t * P : (t + 1) * P]
+                    if j == 0:
+                        nc.tensor.transpose(turned, rows, ident_bf16[:])
+                    else:
+                        nc.tensor.matmul(
+                            out=turned, lhsT=rows, rhs=ident_bf16[:], start=True, stop=True
+                        )
                 turned_states[s, j] = bank[:, j % 2, :]
 
         def add_gates(terms, total):

@@ -33,9 +33,13 @@ CHUNKS = BLOCKS * PASSES
 BATCH = 4
 
 TURN_AHEAD = 4
-QUANTISE_AHEAD = 2
+QUANTISE_AHEAD = 3
 LOAD_AHEAD = 3
 LN_BEHIND = 1
+
+WEIGHTS = slice(0, 1)
+PRODUCTS = slice(1, 2)
+BOTH = slice(0, 2)
 
 
 def tile_multidimensinalgrucell_pb_t_kernel(
@@ -74,8 +78,8 @@ def tile_multidimensinalgrucell_pb_t_kernel(
         rows_pool = ctx.enter_context(tc.tile_pool(name="rows", bufs=LOAD_AHEAD + 1))
         grouped_pool = ctx.enter_context(tc.tile_pool(name="grouped", bufs=TURN_AHEAD))
         pairs = ctx.enter_context(tc.tile_pool(name="pairs", bufs=2))
-        weights_pool = ctx.enter_context(tc.tile_pool(name="weights", bufs=3))
-        sums_pool = ctx.enter_context(tc.tile_pool(name="sums", bufs=2 * BATCH))
+        terms_pool = ctx.enter_context(tc.tile_pool(name="terms", bufs=3))
+        sums_pool = ctx.enter_context(tc.tile_pool(name="sums", bufs=2 * BATCH + 1))
         gate_psum = ctx.enter_context(tc.psum_pool(name="gate_psum", bufs=1))
         state_psum = ctx.enter_context(tc.psum_pool(name="state_psum", bufs=1))
         turn_psum = ctx.enter_context(tc.psum_pool(name="turn_psum", bufs=2))
@@ -104,6 +108,9 @@ def tile_multidimensinalgrucell_pb_t_kernel(
                     out=q_rows[b][:, :, part * UNITS : (part + 1) * UNITS],
                     in_=by_partition(rows)[:, tiles, :],
                 )
+
+        def load_candidate(b):
+            tiles = slice(b * TILES, (b + 1) * TILES)
             nc.sync.dma_start(out=h_rows[b][:], in_=by_partition(h_cand)[:, tiles, :])
 
         load_rows(0)
@@ -123,12 +130,10 @@ def tile_multidimensinalgrucell_pb_t_kernel(
                 out=bias_rows[HALVES * j : HALVES * (j + 1), :],
                 in_=gate_bias[j].rearrange("(h u) -> h u", h=HALVES),
             )
+        load_candidate(0)
         for b in range(1, LOAD_AHEAD):
             load_rows(b)
-
-        bias_turned = turn_psum.tile([P, P], BF16, tag="turn")
-        nc.tensor.transpose(bias_turned[:], bias_rows[:], ident_bf16[:])
-        nc.vector.tensor_copy(out=bias[:], in_=bias_turned[:, 0 : GATES * HALVES])
+            load_candidate(b)
 
         def bias_of(s, j):
             column = HALVES * j + s % HALVES
@@ -140,8 +145,7 @@ def tile_multidimensinalgrucell_pb_t_kernel(
         acc = {}
         turned_states = {}
         top_gate = {}
-        weights = {}
-        weighted = {}
+        terms = {}
         sums = {}
 
         def transpose_q(c):
@@ -209,10 +213,8 @@ def tile_multidimensinalgrucell_pb_t_kernel(
             )
 
         def below_top(s, j):
-            if j == 0:
-                weights[s] = weights_pool.tile([P, GATES, COLS], F32, name="weights")
             nc.vector.scalar_tensor_tensor(
-                out=weights[s][:, j, :],
+                out=terms[s][:, 0, j, :],
                 in0=acc[s, j][:],
                 scalar=bias_of(s, j),
                 in1=top_gate[s][:],
@@ -220,8 +222,9 @@ def tile_multidimensinalgrucell_pb_t_kernel(
                 op1=ALU.subtract,
             )
 
-        def exponential(s, j):
-            nc.scalar.activation(out=weights[s][:, j, :], in_=weights[s][:, j, :], func=ACT.Exp)
+        def exponentials(s, pair):
+            two_gates = terms[s][:, 0, 2 * pair : 2 * pair + 2, :]
+            nc.scalar.activation(out=two_gates, in_=two_gates, func=ACT.Exp)
 
         def transpose_states(s):
             b, h = divmod(s, HALVES)
@@ -234,36 +237,33 @@ def tile_multidimensinalgrucell_pb_t_kernel(
                     else:
                         first = (j - 1) * UNITS + h * P
                         rows = q_rows[b][:, t, first : first + P]
-                    turned = bank[:, j % 2, t * P : (t + 1) * P]
-                    if j == 0:
-                        nc.tensor.transpose(turned, rows, ident_bf16[:])
-                    else:
-                        nc.tensor.matmul(
-                            out=turned, lhsT=rows, rhs=ident_bf16[:], start=True, stop=True
-                        )
-                turned_states[s, j] = bank[:, j % 2, :]
-
-        def add_gates(terms, total):
-            halves = pairs.tile([P, 2, COLS], F32, name="halves")
-            nc.gpsimd.tensor_tensor(
-                out=halves[:], in0=terms[:, 0:2, :], in1=terms[:, 2:4, :], op=ALU.add
-            )
-            nc.gpsimd.tensor_tensor(out=total, in0=halves[:, 0, :], in1=halves[:, 1, :], op=ALU.add)
-
-        def sum_weights(s):
-            sums[s] = sums_pool.tile([P, 2, COLS], F32, name="sums")
-            add_gates(weights[s], sums[s][:, 0, :])
+                    nc.tensor.transpose(bank[:, j % 2, t * P : (t + 1) * P], rows, ident_bf16[:])
+                turned_states[s, j // 2] = bank
 
         def weigh_states(s):
-            weighted[s] = pairs.tile([P, GATES, COLS], F32, name="weighted")
-            for j in range(GATES):
+            for pair in range(GATES // 2):
+                two_gates = slice(2 * pair, 2 * pair + 2)
                 nc.vector.tensor_tensor(
-                    out=weighted[s][:, j, :],
-                    in0=weights[s][:, j, :],
-                    in1=turned_states[s, j],
+                    out=terms[s + 1][:, 1, two_gates, :],
+                    in0=terms[s][:, 0, two_gates, :],
+                    in1=turned_states[s, pair][:],
                     op=ALU.mult,
                 )
-            add_gates(weighted[s], sums[s][:, 1, :])
+
+        def add_gates(engine, s, kinds):
+            halves = pairs.tile([P, 2, 2, COLS], F32, name="halves")
+            engine.tensor_tensor(
+                out=halves[:, kinds, :, :],
+                in0=terms[s][:, kinds, 0:2, :],
+                in1=terms[s][:, kinds, 2:4, :],
+                op=ALU.add,
+            )
+            engine.tensor_tensor(
+                out=sums[s][:, kinds, :],
+                in0=halves[:, kinds, 0, :],
+                in1=halves[:, kinds, 1, :],
+                op=ALU.add,
+            )
 
         def logarithm(s):
             nc.scalar.activation(out=sums[s][:, 0, :], in_=sums[s][:, 0, :], func=ACT.Ln)
@@ -273,7 +273,7 @@ def tile_multidimensinalgrucell_pb_t_kernel(
 
         def normalise(s):
             nc.vector.tensor_tensor(
-                out=sums[s][:, 1, :], in0=sums[s][:, 1, :], in1=sums[s][:, 0, :], op=ALU.mult
+                out=sums[s + 1][:, 1, :], in0=sums[s + 1][:, 1, :], in1=sums[s][:, 0, :], op=ALU.mult
             )
 
         def store(b):
@@ -282,18 +282,21 @@ def tile_multidimensinalgrucell_pb_t_kernel(
                 back = turn_psum.tile([P, TILES, P], F32, name="back", tag="turn")
                 for t in range(TILES):
                     nc.tensor.transpose(
-                        back[:, t, :], sums[b * HALVES + h][:, 1, t * P : (t + 1) * P], ident_f32[:]
+                        back[:, t, :], sums[b * HALVES + h + 1][:, 1, t * P : (t + 1) * P], ident_f32[:]
                     )
                 nc.scalar.copy(out=out_rows[:, :, h * P : (h + 1) * P], in_=back[:])
             nc.sync.dma_start(out=by_partition(out)[:, b * TILES : (b + 1) * TILES, :], in_=out_rows[:])
 
-        for c in range(QUANTISE_AHEAD):
+        for c in range(PASSES):
             transpose_q(c)
             quantise_q(c)
+        bias_turned = turn_psum.tile([P, P], BF16, tag="turn")
+        nc.tensor.transpose(bias_turned[:], bias_rows[:], ident_bf16[:])
+        nc.vector.tensor_copy(out=bias[:], in_=bias_turned[:, 0 : GATES * HALVES])
         for j in range(GATES):
             multiply(0, j)
         first_gate(0)
-        for c in range(QUANTISE_AHEAD, TURN_AHEAD):
+        for c in range(PASSES, TURN_AHEAD):
             transpose_q(c)
         for j in range(1, GATES):
             larger_gate(0, j)
@@ -302,8 +305,9 @@ def tile_multidimensinalgrucell_pb_t_kernel(
         for s in range(STAGES + LN_BEHIND + 3):
             n, step = divmod(s - first_ln, BATCH)
             finishing = 0 <= n
-            if s + QUANTISE_AHEAD < CHUNKS:
-                quantise_q(s + QUANTISE_AHEAD)
+            if s <= STAGES:
+                terms[s] = terms_pool.tile([P, 2, GATES, COLS], F32, name="terms")
+                sums[s] = sums_pool.tile([P, 2, COLS], F32, name="sums")
             for j in range(GATES):
                 if s < STAGES:
                     below_top(s, j)
@@ -311,29 +315,38 @@ def tile_multidimensinalgrucell_pb_t_kernel(
                     multiply(s + 1, j)
                     if j == 0:
                         first_gate(s + 1)
-            if s < STAGES:
-                for j in range(GATES):
-                    exponential(s, j)
-                sum_weights(s)
+                if s < STAGES and j % 2 == 1:
+                    exponentials(s, j // 2)
+            if s == 0 or s == STAGES - 1:
+                add_gates(nc.gpsimd, s, WEIGHTS)
             if 1 <= s <= STAGES:
                 weigh_states(s - 1)
+            for c in range(PASSES if s == 0 else s + QUANTISE_AHEAD, min(s + QUANTISE_AHEAD + 1, CHUNKS)):
+                quantise_q(c)
             if finishing and step >= 2:
                 for h in range(HALVES):
                     normalise(n * BATCH + (step - 2) * HALVES + h)
+            if 1 <= s < STAGES - 1:
+                add_gates(nc.gpsimd, s, BOTH)
+            if s == STAGES - 1:
+                add_gates(nc.gpsimd, s, PRODUCTS)
+            if s == STAGES:
+                add_gates(nc.vector, s, PRODUCTS)
             if s + 1 < STAGES:
                 for j in range(1, GATES):
                     larger_gate(s + 1, j)
-            if s + TURN_AHEAD < CHUNKS:
-                transpose_q(s + TURN_AHEAD)
-            if finishing and step >= 2:
-                store(n * (BATCH // HALVES) + step - 2)
             if s < STAGES:
                 transpose_states(s)
-            if finishing and 1 <= step <= 2:
-                for h in range(HALVES):
-                    reciprocal(n * BATCH + (step - 1) * HALVES + h)
             if finishing and step == 0:
                 for i in range(BATCH):
                     logarithm(n * BATCH + i)
+            if s + TURN_AHEAD < CHUNKS:
+                transpose_q(s + TURN_AHEAD)
+            if finishing and step == 1:
+                for i in range(BATCH):
+                    reciprocal(n * BATCH + i)
+            if finishing and step >= 2:
+                store(n * (BATCH // HALVES) + step - 2)
             if s % HALVES == 1 and s // HALVES + LOAD_AHEAD < BLOCKS:
                 load_rows(s // HALVES + LOAD_AHEAD)
+                load_candidate(s // HALVES + LOAD_AHEAD)

@@ -30,38 +30,16 @@ BLOCKS = ROWS_PER_PARTITION // TILES
 HALVES = UNITS // P
 STAGES = BLOCKS * HALVES
 CHUNKS = BLOCKS * PASSES
-BATCH = 4
 
 TURN_AHEAD = 4
 QUANTISE_AHEAD = 3
 LOAD_AHEAD = 3
-LN_BEHIND = 1
-
-WEIGHTS = slice(0, 1)
-PRODUCTS = slice(1, 2)
-BOTH = slice(0, 2)
 
 
 def tile_multidimensinalgrucell_pb_t_kernel(
-    tc,
-    x,
-    left_state,
-    top_state,
-    diagonal_state,
-    h_cand,
-    w_zi_words,
-    w_zi_scales,
-    b_zi,
-    w_zl_words,
-    w_zl_scales,
-    b_zl,
-    w_zt_words,
-    w_zt_scales,
-    b_zt,
-    w_zd_words,
-    w_zd_scales,
-    b_zd,
-    out,
+    tc, x, left_state, top_state, diagonal_state, h_cand,
+    w_zi_words, w_zi_scales, b_zi, w_zl_words, w_zl_scales, b_zl,
+    w_zt_words, w_zt_scales, b_zt, w_zd_words, w_zd_scales, b_zd, out,
 ):
     nc = tc.nc
     gate_words = (w_zi_words, w_zl_words, w_zt_words, w_zd_words)
@@ -78,10 +56,10 @@ def tile_multidimensinalgrucell_pb_t_kernel(
         rows_pool = ctx.enter_context(tc.tile_pool(name="rows", bufs=LOAD_AHEAD + 1))
         grouped_pool = ctx.enter_context(tc.tile_pool(name="grouped", bufs=TURN_AHEAD))
         pairs = ctx.enter_context(tc.tile_pool(name="pairs", bufs=2))
-        terms_pool = ctx.enter_context(tc.tile_pool(name="terms", bufs=3))
-        sums_pool = ctx.enter_context(tc.tile_pool(name="sums", bufs=2 * BATCH + 1))
+        triples = ctx.enter_context(tc.tile_pool(name="triples", bufs=3))
         gate_psum = ctx.enter_context(tc.psum_pool(name="gate_psum", bufs=1))
         state_psum = ctx.enter_context(tc.psum_pool(name="state_psum", bufs=1))
+        blend_psum = ctx.enter_context(tc.psum_pool(name="blend_psum", bufs=1))
         turn_psum = ctx.enter_context(tc.psum_pool(name="turn_psum", bufs=2))
 
         w_codes = keep.tile([P, GATES, PASSES, UNITS], U32, align_bytes=64)
@@ -90,9 +68,11 @@ def tile_multidimensinalgrucell_pb_t_kernel(
         bias = keep.tile([P, GATES * HALVES], F32)
         ident_bf16 = keep.tile([P, P], BF16)
         ident_f32 = keep.tile([P, P], F32)
+        minus_one = keep.tile([P, COLS], F32)
 
         nc.vector.memset(w_planes[:].bitcast(I32), 0)
         nc.vector.memset(bias_rows[:].bitcast(I32), 0)
+        nc.vector.memset(minus_one[:], -1.0)
         make_identity(nc, ident_f32[:])
         make_identity(nc, ident_bf16[:])
 
@@ -143,15 +123,19 @@ def tile_multidimensinalgrucell_pb_t_kernel(
         q_codes = {}
         q_planes = {}
         acc = {}
-        turned_states = {}
+        states_v = {}
+        states_g = {}
         top_gate = {}
-        terms = {}
-        sums = {}
+        weights = {}
+        products = {}
+        halves = {}
+        total_rows = {}
+        blend = {}
+        out_rows = {}
 
         def transpose_q(c):
             b, g = divmod(c, PASSES)
             grouped[c] = grouped_pool.tile([P, 4 * COLS], BF16, name="grouped", align_bytes=64)
-            banks = []
             for pair in range(TILES // 2):
                 turned = turn_psum.tile([P, 2, 2 * P], F32, name="turned", tag="turn")
                 for i in range(2):
@@ -162,12 +146,10 @@ def tile_multidimensinalgrucell_pb_t_kernel(
                             words[:, WORDS * g + u : WORDS * (g + 1) : 2],
                             ident_f32[:],
                         )
-                banks.append(turned)
-            for pair in range(TILES // 2):
                 side_by_side = grouped[c][:, pair * 8 * P : (pair + 1) * 8 * P].bitcast(F32)
                 nc.scalar.copy(
                     out=side_by_side.rearrange("p (c u) -> p c u", u=2),
-                    in_=banks[pair][:].rearrange("p u c -> p c u"),
+                    in_=turned[:].rearrange("p u c -> p c u"),
                 )
 
         def quantise_q(c):
@@ -204,88 +186,93 @@ def tile_multidimensinalgrucell_pb_t_kernel(
 
         def larger_gate(s, j):
             nc.vector.scalar_tensor_tensor(
-                out=top_gate[s][:],
-                in0=acc[s, j][:],
-                scalar=bias_of(s, j),
-                in1=top_gate[s][:],
-                op0=ALU.add,
-                op1=ALU.max,
+                out=top_gate[s][:], in0=acc[s, j][:], scalar=bias_of(s, j), in1=top_gate[s][:],
+                op0=ALU.add, op1=ALU.max,
             )
 
         def below_top(s, j):
+            if j == 0:
+                weights[s] = triples.tile([P, GATES, COLS], F32, name="weights")
             nc.vector.scalar_tensor_tensor(
-                out=terms[s][:, 0, j, :],
-                in0=acc[s, j][:],
-                scalar=bias_of(s, j),
-                in1=top_gate[s][:],
-                op0=ALU.add,
-                op1=ALU.subtract,
+                out=weights[s][:, j, :], in0=acc[s, j][:], scalar=bias_of(s, j), in1=top_gate[s][:],
+                op0=ALU.add, op1=ALU.subtract,
             )
 
         def exponentials(s, pair):
-            two_gates = terms[s][:, 0, 2 * pair : 2 * pair + 2, :]
+            two_gates = weights[s][:, 2 * pair : 2 * pair + 2, :]
             nc.scalar.activation(out=two_gates, in_=two_gates, func=ACT.Exp)
 
-        def transpose_states(s):
+        def state_rows(s, j, t):
             b, h = divmod(s, HALVES)
-            for j in range(GATES):
-                if j % 2 == 0:
-                    bank = state_psum.tile([P, 2, COLS], BF16, name="states%d" % (j // 2))
+            if j == 0:
+                return h_rows[b][:, t, h * P : (h + 1) * P]
+            first = (j - 1) * UNITS + h * P
+            return q_rows[b][:, t, first : first + P]
+
+        def transpose_states_v(s):
+            states_v[s] = state_psum.tile([P, 2, COLS], BF16, name="states_v")
+            for j in range(2):
                 for t in range(TILES):
-                    if j == 0:
-                        rows = h_rows[b][:, t, h * P : (h + 1) * P]
-                    else:
-                        first = (j - 1) * UNITS + h * P
-                        rows = q_rows[b][:, t, first : first + P]
-                    nc.tensor.transpose(bank[:, j % 2, t * P : (t + 1) * P], rows, ident_bf16[:])
-                turned_states[s, j // 2] = bank
+                    nc.tensor.transpose(states_v[s][:, j, t * P : (t + 1) * P], state_rows(s, j, t), ident_bf16[:])
 
-        def weigh_states(s):
-            for pair in range(GATES // 2):
-                two_gates = slice(2 * pair, 2 * pair + 2)
-                nc.vector.tensor_tensor(
-                    out=terms[s + 1][:, 1, two_gates, :],
-                    in0=terms[s][:, 0, two_gates, :],
-                    in1=turned_states[s, pair][:],
-                    op=ALU.mult,
-                )
+        def transpose_states_g(s):
+            bank = turn_psum.tile([P, 2, COLS], BF16, name="states_t", tag="turn")
+            for j in range(2):
+                for t in range(TILES):
+                    nc.tensor.transpose(bank[:, j, t * P : (t + 1) * P], state_rows(s, 2 + j, t), ident_bf16[:])
+            states_g[s] = pairs.tile([P, 2, COLS], BF16, name="states_g")
+            nc.scalar.copy(out=states_g[s][:], in_=bank[:])
 
-        def add_gates(engine, s, kinds):
-            halves = pairs.tile([P, 2, 2, COLS], F32, name="halves")
-            engine.tensor_tensor(
-                out=halves[:, kinds, :, :],
-                in0=terms[s][:, kinds, 0:2, :],
-                in1=terms[s][:, kinds, 2:4, :],
-                op=ALU.add,
-            )
-            engine.tensor_tensor(
-                out=sums[s][:, kinds, :],
-                in0=halves[:, kinds, 0, :],
-                in1=halves[:, kinds, 1, :],
-                op=ALU.add,
+        def weigh_v(s):
+            products[s] = triples.tile([P, GATES, COLS], F32, name="products")
+            nc.vector.tensor_tensor(
+                out=products[s][:, 0:2, :], in0=weights[s][:, 0:2, :], in1=states_v[s][:], op=ALU.mult
             )
 
-        def logarithm(s):
-            nc.scalar.activation(out=sums[s][:, 0, :], in_=sums[s][:, 0, :], func=ACT.Ln)
+        def weigh_g(s):
+            nc.gpsimd.tensor_tensor(
+                out=products[s][:, 2:4, :], in0=weights[s][:, 2:4, :], in1=states_g[s][:], op=ALU.mult
+            )
 
-        def reciprocal(s):
-            nc.scalar.activation(out=sums[s][:, 0, :], in_=sums[s][:, 0, :], func=ACT.Exp, scale=-1.0)
+        def add_pairs(s):
+            halves[s] = pairs.tile([P, 2, COLS], F32, name="halves")
+            nc.gpsimd.tensor_tensor(
+                out=halves[s][:], in0=weights[s][:, 0:2, :], in1=weights[s][:, 2:4, :], op=ALU.add
+            )
+
+        def sum_weights(s):
+            bank = turn_psum.tile([P, TILES, P], F32, name="total_t", tag="turn")
+            for t in range(TILES):
+                for i in range(2):
+                    nc.tensor.matmul(
+                        out=bank[:, t, :], lhsT=halves[s][:, i, t * P : (t + 1) * P], rhs=ident_f32[:],
+                        is_transpose=True, start=(i == 0), stop=(i == 1),
+                    )
+            total_rows[s] = triples.tile([P, COLS], F32, name="total_rows")
+            nc.scalar.copy(out=total_rows[s][:], in_=bank[:].rearrange("p t u -> p (t u)"))
+
+        def invert(s):
+            nc.gpsimd.tensor_tensor(out=total_rows[s][:], in0=total_rows[s][:], in1=minus_one[:], op=ALU.pow)
+
+        def sum_products(s):
+            blend[s] = blend_psum.tile([P, TILES, P], F32, name="blend")
+            for t in range(TILES):
+                for j in range(GATES):
+                    nc.tensor.matmul(
+                        out=blend[s][:, t, :], lhsT=products[s][:, j, t * P : (t + 1) * P], rhs=ident_f32[:],
+                        is_transpose=True, start=(j == 0), stop=(j == GATES - 1),
+                    )
 
         def normalise(s):
+            b, h = divmod(s, HALVES)
+            if h == 0:
+                out_rows[b] = pairs.tile([P, TILES, UNITS], F32, name="out_rows")
             nc.vector.tensor_tensor(
-                out=sums[s + 1][:, 1, :], in0=sums[s + 1][:, 1, :], in1=sums[s][:, 0, :], op=ALU.mult
+                out=out_rows[b][:, :, h * P : (h + 1) * P], in0=blend[s][:],
+                in1=total_rows[s][:].rearrange("p (t u) -> p t u", t=TILES), op=ALU.mult,
             )
-
-        def store(b):
-            out_rows = pairs.tile([P, TILES, UNITS], F32, name="out_rows")
-            for h in range(HALVES):
-                back = turn_psum.tile([P, TILES, P], F32, name="back", tag="turn")
-                for t in range(TILES):
-                    nc.tensor.transpose(
-                        back[:, t, :], sums[b * HALVES + h + 1][:, 1, t * P : (t + 1) * P], ident_f32[:]
-                    )
-                nc.scalar.copy(out=out_rows[:, :, h * P : (h + 1) * P], in_=back[:])
-            nc.sync.dma_start(out=by_partition(out)[:, b * TILES : (b + 1) * TILES, :], in_=out_rows[:])
+            if h == HALVES - 1:
+                nc.sync.dma_start(out=by_partition(out)[:, b * TILES : (b + 1) * TILES, :], in_=out_rows[b][:])
 
         for c in range(PASSES):
             transpose_q(c)
@@ -301,52 +288,44 @@ def tile_multidimensinalgrucell_pb_t_kernel(
         for j in range(1, GATES):
             larger_gate(0, j)
 
-        first_ln = BATCH - 1 + LN_BEHIND
-        for s in range(STAGES + LN_BEHIND + 3):
-            n, step = divmod(s - first_ln, BATCH)
-            finishing = 0 <= n
-            if s <= STAGES:
-                terms[s] = terms_pool.tile([P, 2, GATES, COLS], F32, name="terms")
-                sums[s] = sums_pool.tile([P, 2, COLS], F32, name="sums")
-            for j in range(GATES):
-                if s < STAGES:
-                    below_top(s, j)
-                if s + 1 < STAGES:
+        def live(s):
+            return 0 <= s < STAGES
+
+        for s in range(STAGES + 3):
+            if live(s):
+                below_top(s, 0)
+                below_top(s, 1)
+                exponentials(s, 0)
+                below_top(s, 2)
+                below_top(s, 3)
+            if live(s - 1):
+                sum_weights(s - 1)
+            if live(s + 1):
+                for j in range(GATES):
                     multiply(s + 1, j)
                     if j == 0:
                         first_gate(s + 1)
-                if s < STAGES and j % 2 == 1:
-                    exponentials(s, j // 2)
-            if s == 0 or s == STAGES - 1:
-                add_gates(nc.gpsimd, s, WEIGHTS)
-            if 1 <= s <= STAGES:
-                weigh_states(s - 1)
+            if live(s):
+                exponentials(s, 1)
+            if live(s - 2):
+                normalise(s - 2)
+            if live(s - 1):
+                weigh_v(s - 1)
+                weigh_g(s - 1)
+                invert(s - 1)
             for c in range(PASSES if s == 0 else s + QUANTISE_AHEAD, min(s + QUANTISE_AHEAD + 1, CHUNKS)):
                 quantise_q(c)
-            if finishing and step >= 2:
-                for h in range(HALVES):
-                    normalise(n * BATCH + (step - 2) * HALVES + h)
-            if 1 <= s < STAGES - 1:
-                add_gates(nc.gpsimd, s, BOTH)
-            if s == STAGES - 1:
-                add_gates(nc.gpsimd, s, PRODUCTS)
-            if s == STAGES:
-                add_gates(nc.vector, s, PRODUCTS)
-            if s + 1 < STAGES:
+            if live(s + 1):
                 for j in range(1, GATES):
                     larger_gate(s + 1, j)
-            if s < STAGES:
-                transpose_states(s)
-            if finishing and step == 0:
-                for i in range(BATCH):
-                    logarithm(n * BATCH + i)
+            if live(s):
+                add_pairs(s)
+                transpose_states_v(s)
+                transpose_states_g(s)
+            if live(s - 1):
+                sum_products(s - 1)
             if s + TURN_AHEAD < CHUNKS:
                 transpose_q(s + TURN_AHEAD)
-            if finishing and step == 1:
-                for i in range(BATCH):
-                    reciprocal(n * BATCH + i)
-            if finishing and step >= 2:
-                store(n * (BATCH // HALVES) + step - 2)
             if s % HALVES == 1 and s // HALVES + LOAD_AHEAD < BLOCKS:
                 load_rows(s // HALVES + LOAD_AHEAD)
                 load_candidate(s // HALVES + LOAD_AHEAD)

@@ -34,6 +34,7 @@ CHUNKS = BLOCKS * PASSES
 TURN_AHEAD = 4
 QUANTISE_AHEAD = 3
 LOAD_AHEAD = 3
+BATCH = 4
 
 
 def tile_multidimensinalgrucell_pb_t_kernel(
@@ -54,9 +55,11 @@ def tile_multidimensinalgrucell_pb_t_kernel(
         ctx.enter_context(tc.manual_schedule())
         keep = ctx.enter_context(tc.tile_pool(name="keep", bufs=1))
         rows_pool = ctx.enter_context(tc.tile_pool(name="rows", bufs=LOAD_AHEAD + 1))
-        grouped_pool = ctx.enter_context(tc.tile_pool(name="grouped", bufs=TURN_AHEAD))
+        grouped_pool = ctx.enter_context(tc.tile_pool(name="grouped", bufs=2))
         pairs = ctx.enter_context(tc.tile_pool(name="pairs", bufs=2))
         triples = ctx.enter_context(tc.tile_pool(name="triples", bufs=3))
+        fours = ctx.enter_context(tc.tile_pool(name="fours", bufs=4))
+        waiting = ctx.enter_context(tc.tile_pool(name="waiting", bufs=BATCH + 2))
         gate_psum = ctx.enter_context(tc.psum_pool(name="gate_psum", bufs=1))
         state_psum = ctx.enter_context(tc.psum_pool(name="state_psum", bufs=1))
         blend_psum = ctx.enter_context(tc.psum_pool(name="blend_psum", bufs=1))
@@ -68,11 +71,9 @@ def tile_multidimensinalgrucell_pb_t_kernel(
         bias = keep.tile([P, GATES * HALVES], F32)
         ident_bf16 = keep.tile([P, P], BF16)
         ident_f32 = keep.tile([P, P], F32)
-        minus_one = keep.tile([P, COLS], F32)
 
         nc.vector.memset(w_planes[:].bitcast(I32), 0)
         nc.vector.memset(bias_rows[:].bitcast(I32), 0)
-        nc.vector.memset(minus_one[:], -1.0)
         make_identity(nc, ident_f32[:])
         make_identity(nc, ident_bf16[:])
 
@@ -120,6 +121,8 @@ def tile_multidimensinalgrucell_pb_t_kernel(
             return bias[:, column : column + 1]
 
         grouped = {}
+        turned = {}
+        states_t = {}
         q_codes = {}
         q_planes = {}
         acc = {}
@@ -130,37 +133,45 @@ def tile_multidimensinalgrucell_pb_t_kernel(
         products = {}
         halves = {}
         total_rows = {}
+        total = {}
+        log_rows = {}
         blend = {}
         out_rows = {}
 
-        def transpose_q(c):
+        def turn_q(c, pair):
             b, g = divmod(c, PASSES)
-            grouped[c] = grouped_pool.tile([P, 4 * COLS], BF16, name="grouped", align_bytes=64)
-            for pair in range(TILES // 2):
-                turned = turn_psum.tile([P, 2, 2 * P], F32, name="turned", tag="turn")
-                for i in range(2):
-                    words = q_rows[b][:, 2 * pair + i, :].bitcast(F32)
-                    for u in range(2):
-                        nc.tensor.transpose(
-                            turned[:, u, i * P : (i + 1) * P],
-                            words[:, WORDS * g + u : WORDS * (g + 1) : 2],
-                            ident_f32[:],
-                        )
-                side_by_side = grouped[c][:, pair * 8 * P : (pair + 1) * 8 * P].bitcast(F32)
-                nc.scalar.copy(
-                    out=side_by_side.rearrange("p (c u) -> p c u", u=2),
-                    in_=turned[:].rearrange("p u c -> p c u"),
-                )
+            turned[c, pair] = turn_psum.tile([P, 2, 2 * P], F32, name="turned", tag="turn")
+            for i in range(2):
+                words = q_rows[b][:, 2 * pair + i, :].bitcast(F32)
+                for u in range(2):
+                    nc.tensor.transpose(
+                        turned[c, pair][:, u, i * P : (i + 1) * P],
+                        words[:, WORDS * g + u : WORDS * (g + 1) : 2],
+                        ident_f32[:],
+                    )
 
-        def quantise_q(c):
+        def group_q(c, pair):
             b, g = divmod(c, PASSES)
-            if g == 0:
-                q_codes[b] = pairs.tile([P, PASSES, COLS], U32, name="q_codes", align_bytes=64)
-                q_planes[b] = pairs.tile([P, PASSES, COLS], U8, name="q_planes", align_bytes=64)
+            if g == 0 and pair == 0:
+                grouped[b] = grouped_pool.tile([P, PASSES, 4 * COLS], BF16, name="grouped", align_bytes=64)
+            side_by_side = grouped[b][:, g, pair * 8 * P : (pair + 1) * 8 * P].bitcast(F32)
+            nc.scalar.copy(
+                out=side_by_side.rearrange("p (c u) -> p c u", u=2),
+                in_=turned[c, pair][:].rearrange("p u c -> p c u"),
+            )
+
+        def transpose_q(c):
+            for pair in range(TILES // 2):
+                turn_q(c, pair)
+                group_q(c, pair)
+
+        def quantise_q(b):
+            q_codes[b] = pairs.tile([P, PASSES, COLS], U32, name="q_codes", align_bytes=64)
+            q_planes[b] = pairs.tile([P, PASSES, COLS], U8, name="q_planes", align_bytes=64)
             nc.vector.quantize_mx(
-                out=q_codes[b][:, g, :].bitcast(FP8X4),
-                scales=q_planes[b][:, g, :],
-                in_=grouped[c][:],
+                out=q_codes[b][:].rearrange("p g c -> p (g c)").bitcast(FP8X4),
+                scales=q_planes[b][:].rearrange("p g c -> p (g c)"),
+                in_=grouped[b][:].rearrange("p g c -> p (g c)"),
             )
 
         def multiply(s, j):
@@ -192,7 +203,7 @@ def tile_multidimensinalgrucell_pb_t_kernel(
 
         def below_top(s, j):
             if j == 0:
-                weights[s] = triples.tile([P, GATES, COLS], F32, name="weights")
+                weights[s] = fours.tile([P, GATES, COLS], F32, name="weights")
             nc.vector.scalar_tensor_tensor(
                 out=weights[s][:, j, :], in0=acc[s, j][:], scalar=bias_of(s, j), in1=top_gate[s][:],
                 op0=ALU.add, op1=ALU.subtract,
@@ -216,15 +227,17 @@ def tile_multidimensinalgrucell_pb_t_kernel(
                     nc.tensor.transpose(states_v[s][:, j, t * P : (t + 1) * P], state_rows(s, j, t), ident_bf16[:])
 
         def transpose_states_g(s):
-            bank = turn_psum.tile([P, 2, COLS], BF16, name="states_t", tag="turn")
+            states_t[s] = turn_psum.tile([P, 2, COLS], BF16, name="states_t", tag="turn")
             for j in range(2):
                 for t in range(TILES):
-                    nc.tensor.transpose(bank[:, j, t * P : (t + 1) * P], state_rows(s, 2 + j, t), ident_bf16[:])
+                    nc.tensor.transpose(states_t[s][:, j, t * P : (t + 1) * P], state_rows(s, 2 + j, t), ident_bf16[:])
+
+        def copy_states_g(s):
             states_g[s] = pairs.tile([P, 2, COLS], BF16, name="states_g")
-            nc.scalar.copy(out=states_g[s][:], in_=bank[:])
+            nc.scalar.copy(out=states_g[s][:], in_=states_t[s][:])
 
         def weigh_v(s):
-            products[s] = triples.tile([P, GATES, COLS], F32, name="products")
+            products[s] = waiting.tile([P, GATES, COLS], F32, name="products")
             nc.vector.tensor_tensor(
                 out=products[s][:, 0:2, :], in0=weights[s][:, 0:2, :], in1=states_v[s][:], op=ALU.mult
             )
@@ -240,19 +253,21 @@ def tile_multidimensinalgrucell_pb_t_kernel(
                 out=halves[s][:], in0=weights[s][:, 0:2, :], in1=weights[s][:, 2:4, :], op=ALU.add
             )
 
-        def sum_weights(s):
-            bank = turn_psum.tile([P, TILES, P], F32, name="total_t", tag="turn")
+        def add_halves(s):
+            total[s] = waiting.tile([P, COLS], F32, name="total")
+            nc.gpsimd.tensor_tensor(out=total[s][:], in0=halves[s][:, 0, :], in1=halves[s][:, 1, :], op=ALU.add)
+
+        def logarithm(s):
+            nc.scalar.activation(out=total[s][:], in_=total[s][:], func=ACT.Ln)
+
+        def turn_log(s):
+            log_rows[s] = turn_psum.tile([P, COLS], F32, name="log_t", tag="turn")
             for t in range(TILES):
-                for i in range(2):
-                    nc.tensor.matmul(
-                        out=bank[:, t, :], lhsT=halves[s][:, i, t * P : (t + 1) * P], rhs=ident_f32[:],
-                        is_transpose=True, start=(i == 0), stop=(i == 1),
-                    )
-            total_rows[s] = triples.tile([P, COLS], F32, name="total_rows")
-            nc.scalar.copy(out=total_rows[s][:], in_=bank[:].rearrange("p t u -> p (t u)"))
+                nc.tensor.transpose(log_rows[s][:, t * P : (t + 1) * P], total[s][:, t * P : (t + 1) * P], ident_f32[:])
 
         def invert(s):
-            nc.gpsimd.tensor_tensor(out=total_rows[s][:], in0=total_rows[s][:], in1=minus_one[:], op=ALU.pow)
+            total_rows[s] = triples.tile([P, COLS], F32, name="total_rows")
+            nc.scalar.activation(out=total_rows[s][:], in_=log_rows[s][:], func=ACT.Exp, scale=-1.0)
 
         def sum_products(s):
             blend[s] = blend_psum.tile([P, TILES, P], F32, name="blend")
@@ -274,58 +289,76 @@ def tile_multidimensinalgrucell_pb_t_kernel(
             if h == HALVES - 1:
                 nc.sync.dma_start(out=by_partition(out)[:, b * TILES : (b + 1) * TILES, :], in_=out_rows[b][:])
 
-        for c in range(PASSES):
-            transpose_q(c)
-            quantise_q(c)
+        transpose_q(0)
+        transpose_q(1)
+        quantise_q(0)
         bias_turned = turn_psum.tile([P, P], BF16, tag="turn")
         nc.tensor.transpose(bias_turned[:], bias_rows[:], ident_bf16[:])
         nc.vector.tensor_copy(out=bias[:], in_=bias_turned[:, 0 : GATES * HALVES])
         for j in range(GATES):
             multiply(0, j)
         first_gate(0)
-        for c in range(PASSES, TURN_AHEAD):
-            transpose_q(c)
+        transpose_q(2)
+        transpose_q(3)
         for j in range(1, GATES):
             larger_gate(0, j)
 
         def live(s):
             return 0 <= s < STAGES
 
-        for s in range(STAGES + 3):
-            if live(s):
-                below_top(s, 0)
-                below_top(s, 1)
-                exponentials(s, 0)
-                below_top(s, 2)
-                below_top(s, 3)
-            if live(s - 1):
-                sum_weights(s - 1)
-            if live(s + 1):
-                for j in range(GATES):
+        LAG = BATCH + 1
+        for s in range(STAGES + LAG + 2):
+            a = s - LAG
+            burst = s % BATCH == 0 and live(s - 1)
+            after = s % BATCH == 1 and live(s - 2)
+            quantising = s % 2 == 0 and s // 2 + 1 < BLOCKS
+            c = s + TURN_AHEAD
+            if live(a) and not after:
+                invert(a)
+            for j in range(GATES):
+                if live(s):
+                    below_top(s, j)
+                if live(s + 1):
                     multiply(s + 1, j)
-                    if j == 0:
-                        first_gate(s + 1)
-            if live(s):
-                exponentials(s, 1)
-            if live(s - 2):
-                normalise(s - 2)
+                if j == 0 and live(s + 1):
+                    first_gate(s + 1)
+                if j == 0 and after:
+                    logarithm(s - 3)
+                    logarithm(s - 2)
+                    invert(a)
+                if live(s) and j % 2 == 1:
+                    exponentials(s, j // 2)
+            if live(a - 1):
+                normalise(a - 1)
             if live(s - 1):
                 weigh_v(s - 1)
                 weigh_g(s - 1)
-                invert(s - 1)
-            for c in range(PASSES if s == 0 else s + QUANTISE_AHEAD, min(s + QUANTISE_AHEAD + 1, CHUNKS)):
-                quantise_q(c)
+            if quantising:
+                quantise_q(s // 2 + 1)
             if live(s + 1):
-                for j in range(1, GATES):
-                    larger_gate(s + 1, j)
+                larger_gate(s + 1, 1)
+                larger_gate(s + 1, 2)
+                larger_gate(s + 1, 3)
+            if c < CHUNKS:
+                turn_q(c, 0)
+                group_q(c, 0)
+            if burst:
+                logarithm(s - 4)
+            if live(a):
+                sum_products(a)
+            if c < CHUNKS:
+                turn_q(c, 1)
+                group_q(c, 1)
+            if burst:
+                logarithm(s - 3)
             if live(s):
-                add_pairs(s)
                 transpose_states_v(s)
                 transpose_states_g(s)
-            if live(s - 1):
-                sum_products(s - 1)
-            if s + TURN_AHEAD < CHUNKS:
-                transpose_q(s + TURN_AHEAD)
+                copy_states_g(s)
+                add_pairs(s)
+                add_halves(s)
+            if live(a + 1):
+                turn_log(a + 1)
             if s % HALVES == 1 and s // HALVES + LOAD_AHEAD < BLOCKS:
                 load_rows(s // HALVES + LOAD_AHEAD)
                 load_candidate(s // HALVES + LOAD_AHEAD)

@@ -220,26 +220,35 @@ def tile_multidimensinalgrucell_pb_t_kernel(
             first = (j - 1) * UNITS + h * P
             return q_rows[b][:, t, first : first + P]
 
-        def transpose_states_v(s):
-            states_v[s] = state_psum.tile([P, 2, COLS], BF16, name="states_v")
+        spare_banks = [0]
+
+        def spare(shape, dtype):
+            spare_banks[0] += 1
+            return gate_psum.tile(shape, dtype, name="acc%d" % (spare_banks[0] % GATES))
+
+        def transpose_states(s, pair, bank):
             for j in range(2):
                 for t in range(TILES):
-                    nc.tensor.transpose(states_v[s][:, j, t * P : (t + 1) * P], state_rows(s, j, t), ident_bf16[:])
+                    nc.tensor.transpose(bank[:, j, t * P : (t + 1) * P], state_rows(s, 2 * pair + j, t), ident_bf16[:])
+            states_t[s, pair] = bank
+
+        def transpose_states_v(s):
+            transpose_states(s, 0, state_psum.tile([P, 2, COLS], BF16, name="states_v"))
 
         def transpose_states_g(s):
-            states_t[s] = turn_psum.tile([P, 2, COLS], BF16, name="states_t", tag="turn")
-            for j in range(2):
-                for t in range(TILES):
-                    nc.tensor.transpose(states_t[s][:, j, t * P : (t + 1) * P], state_rows(s, 2 + j, t), ident_bf16[:])
+            transpose_states(s, 1, turn_psum.tile([P, 2, COLS], BF16, name="states_t", tag="turn"))
 
         def copy_states_g(s):
-            states_g[s] = pairs.tile([P, 2, COLS], BF16, name="states_g")
-            nc.scalar.copy(out=states_g[s][:], in_=states_t[s][:])
+            states_g[s] = fours.tile([P, 2, COLS], BF16, name="states_g")
+            nc.scalar.copy(out=states_g[s][:], in_=states_t[s, 1][:])
 
-        def weigh_v(s):
+        def open_products(s):
             products[s] = waiting.tile([P, GATES, COLS], F32, name="products")
+
+        def weigh_v(s, pair=0):
+            two_gates = slice(2 * pair, 2 * pair + 2)
             nc.vector.tensor_tensor(
-                out=products[s][:, 0:2, :], in0=weights[s][:, 0:2, :], in1=states_v[s][:], op=ALU.mult
+                out=products[s][:, two_gates, :], in0=weights[s][:, two_gates, :], in1=states_t[s, pair][:], op=ALU.mult
             )
 
         def weigh_g(s):
@@ -247,15 +256,15 @@ def tile_multidimensinalgrucell_pb_t_kernel(
                 out=products[s][:, 2:4, :], in0=weights[s][:, 2:4, :], in1=states_g[s][:], op=ALU.mult
             )
 
-        def add_pairs(s):
+        def add_pairs(s, engine):
             halves[s] = pairs.tile([P, 2, COLS], F32, name="halves")
-            nc.gpsimd.tensor_tensor(
+            engine.tensor_tensor(
                 out=halves[s][:], in0=weights[s][:, 0:2, :], in1=weights[s][:, 2:4, :], op=ALU.add
             )
 
-        def add_halves(s):
+        def add_halves(s, engine):
             total[s] = waiting.tile([P, COLS], F32, name="total")
-            nc.gpsimd.tensor_tensor(out=total[s][:], in0=halves[s][:, 0, :], in1=halves[s][:, 1, :], op=ALU.add)
+            engine.tensor_tensor(out=total[s][:], in0=halves[s][:, 0, :], in1=halves[s][:, 1, :], op=ALU.add)
 
         def logarithm(s):
             nc.scalar.activation(out=total[s][:], in_=total[s][:], func=ACT.Ln)
@@ -266,11 +275,14 @@ def tile_multidimensinalgrucell_pb_t_kernel(
                 nc.tensor.transpose(log_rows[s][:, t * P : (t + 1) * P], total[s][:, t * P : (t + 1) * P], ident_f32[:])
 
         def invert(s):
-            total_rows[s] = triples.tile([P, COLS], F32, name="total_rows")
+            total_rows[s] = fours.tile([P, COLS], F32, name="total_rows")
             nc.scalar.activation(out=total_rows[s][:], in_=log_rows[s][:], func=ACT.Exp, scale=-1.0)
 
-        def sum_products(s):
-            blend[s] = blend_psum.tile([P, TILES, P], F32, name="blend")
+        def sum_products(s, in_spare=False):
+            if in_spare:
+                blend[s] = spare([P, TILES, P], F32)
+            else:
+                blend[s] = blend_psum.tile([P, TILES, P], F32, name="blend")
             for t in range(TILES):
                 for j in range(GATES):
                     nc.tensor.matmul(
@@ -281,12 +293,15 @@ def tile_multidimensinalgrucell_pb_t_kernel(
         def normalise(s):
             b, h = divmod(s, HALVES)
             if h == 0:
-                out_rows[b] = pairs.tile([P, TILES, UNITS], F32, name="out_rows")
+                out_rows[b] = triples.tile([P, TILES, UNITS], F32, name="out_rows")
             nc.vector.tensor_tensor(
                 out=out_rows[b][:, :, h * P : (h + 1) * P], in0=blend[s][:],
                 in1=total_rows[s][:].rearrange("p (t u) -> p t u", t=TILES), op=ALU.mult,
             )
-            if h == HALVES - 1:
+            if b == BLOCKS - 1:
+                units = slice(h * P, (h + 1) * P)
+                nc.sync.dma_start(out=by_partition(out)[:, b * TILES : (b + 1) * TILES, units], in_=out_rows[b][:, :, units])
+            elif h == HALVES - 1:
                 nc.sync.dma_start(out=by_partition(out)[:, b * TILES : (b + 1) * TILES, :], in_=out_rows[b][:])
 
         transpose_q(0)
@@ -307,7 +322,8 @@ def tile_multidimensinalgrucell_pb_t_kernel(
             return 0 <= s < STAGES
 
         LAG = BATCH + 1
-        for s in range(STAGES + LAG + 2):
+        last = STAGES - 1
+        for s in range(STAGES):
             a = s - LAG
             burst = s % BATCH == 0 and live(s - 1)
             after = s % BATCH == 1 and live(s - 2)
@@ -315,9 +331,11 @@ def tile_multidimensinalgrucell_pb_t_kernel(
             c = s + TURN_AHEAD
             if live(a) and not after:
                 invert(a)
+            if s == last:
+                turn_log(a + 1)
+                invert(a + 1)
             for j in range(GATES):
-                if live(s):
-                    below_top(s, j)
+                below_top(s, j)
                 if live(s + 1):
                     multiply(s + 1, j)
                 if j == 0 and live(s + 1):
@@ -326,11 +344,12 @@ def tile_multidimensinalgrucell_pb_t_kernel(
                     logarithm(s - 3)
                     logarithm(s - 2)
                     invert(a)
-                if live(s) and j % 2 == 1:
+                if j % 2 == 1:
                     exponentials(s, j // 2)
             if live(a - 1):
                 normalise(a - 1)
-            if live(s - 1):
+            if live(s - 1) and s < last:
+                open_products(s - 1)
                 weigh_v(s - 1)
                 weigh_g(s - 1)
             if quantising:
@@ -351,14 +370,46 @@ def tile_multidimensinalgrucell_pb_t_kernel(
                 group_q(c, 1)
             if burst:
                 logarithm(s - 3)
-            if live(s):
+            if s < last:
                 transpose_states_v(s)
+                add_pairs(s, nc.gpsimd)
+                add_halves(s, nc.gpsimd)
+            if s < last - 1:
                 transpose_states_g(s)
                 copy_states_g(s)
-                add_pairs(s)
-                add_halves(s)
-            if live(a + 1):
+            if s < last and live(a + 1):
                 turn_log(a + 1)
             if s % HALVES == 1 and s // HALVES + LOAD_AHEAD < BLOCKS:
                 load_rows(s // HALVES + LOAD_AHEAD)
                 load_candidate(s // HALVES + LOAD_AHEAD)
+
+        summed = last - LAG
+        batch = list(range(STAGES - BATCH, STAGES))
+        add_pairs(last, nc.vector)
+        add_halves(last, nc.vector)
+        for s in batch:
+            logarithm(s)
+        transpose_states(last - 1, 1, spare([P, 2, COLS], BF16))
+        transpose_states(last, 0, spare([P, 2, COLS], BF16))
+        transpose_states(last, 1, spare([P, 2, COLS], BF16))
+        normalise(summed)
+        turn_log(batch[0])
+        turn_log(batch[1])
+        sum_products(summed + 1)
+        sum_products(batch[0], in_spare=True)
+        for s in (last - 1, last):
+            open_products(s)
+            weigh_v(s, 0)
+            weigh_v(s, 1)
+        normalise(summed + 1)
+        sum_products(batch[1], in_spare=True)
+        invert(batch[0])
+        invert(batch[1])
+        turn_log(batch[2])
+        turn_log(batch[3])
+        sum_products(batch[2], in_spare=True)
+        sum_products(batch[3], in_spare=True)
+        invert(batch[2])
+        invert(batch[3])
+        for s in batch:
+            normalise(s)

@@ -238,9 +238,17 @@ def tile_multidimensinalgrucell_pb_t_kernel(
         def transpose_states_g(s):
             transpose_states(s, 1, turn_psum.tile([P, 2, COLS], BF16, name="states_t", tag="turn"))
 
+        def copy_state_l(s):
+            states_g[s] = fours.tile([P, 3, COLS], BF16, name="states_g")
+            nc.scalar.copy(out=states_g[s][:, 0, :], in_=states_t[s, 0][:, 1, :])
+
         def copy_states_g(s):
-            states_g[s] = fours.tile([P, 2, COLS], BF16, name="states_g")
-            nc.scalar.copy(out=states_g[s][:], in_=states_t[s, 1][:])
+            nc.scalar.copy(out=states_g[s][:, 1:3, :], in_=states_t[s, 1][:])
+
+        def weigh_first(s):
+            nc.vector.tensor_tensor(
+                out=products[s][:, 0, :], in0=weights[s][:, 0, :], in1=states_t[s, 0][:, 0, :], op=ALU.mult
+            )
 
         def open_products(s):
             products[s] = waiting.tile([P, GATES, COLS], F32, name="products")
@@ -253,7 +261,7 @@ def tile_multidimensinalgrucell_pb_t_kernel(
 
         def weigh_g(s):
             nc.gpsimd.tensor_tensor(
-                out=products[s][:, 2:4, :], in0=weights[s][:, 2:4, :], in1=states_g[s][:], op=ALU.mult
+                out=products[s][:, 1:4, :], in0=weights[s][:, 1:4, :], in1=states_g[s][:], op=ALU.mult
             )
 
         def add_pairs(s, engine):
@@ -350,7 +358,7 @@ def tile_multidimensinalgrucell_pb_t_kernel(
                 normalise(a - 1)
             if live(s - 1) and s < last:
                 open_products(s - 1)
-                weigh_v(s - 1)
+                weigh_first(s - 1)
                 weigh_g(s - 1)
             if quantising:
                 quantise_q(s // 2 + 1)
@@ -375,6 +383,7 @@ def tile_multidimensinalgrucell_pb_t_kernel(
                 add_pairs(s, nc.gpsimd)
                 add_halves(s, nc.gpsimd)
             if s < last - 1:
+                copy_state_l(s)
                 transpose_states_g(s)
                 copy_states_g(s)
             if s < last and live(a + 1):

from contextlib import ExitStack

import concourse.mybir as mybir
from concourse.masks import make_identity

FLOPS = 2 * 4096 * 1024 * 1024

F32 = mybir.dt.float32
BF16 = mybir.dt.bfloat16
I32 = mybir.dt.int32
U32 = mybir.dt.uint32
U8 = mybir.dt.uint8
FP8X4 = mybir.dt.float8_e4m3fn_x4
ALU = mybir.AluOpType
ACT = mybir.ActivationFunctionType

P = 128
ROWS = 4096
UNITS = 256
K = 1024
GATES = 4
K_PASS = 512
PASSES = K // K_PASS
WORDS = K_PASS // 2

ROWS_PER_PARTITION = ROWS // P
TILES = 4
COLS = TILES * P
BLOCKS = ROWS_PER_PARTITION // TILES
HALVES = UNITS // P
STAGES = BLOCKS * HALVES
CHUNKS = BLOCKS * PASSES

TURN_AHEAD = 4
QUANTISE_AHEAD = 3
LOAD_AHEAD = 3
BATCH = 4


def tile_multidimensinalgrucell_pb_t_kernel(
    tc, x, left_state, top_state, diagonal_state, h_cand,
    w_zi_words, w_zi_scales, b_zi, w_zl_words, w_zl_scales, b_zl,
    w_zt_words, w_zt_scales, b_zt, w_zd_words, w_zd_scales, b_zd, out,
):
    nc = tc.nc
    gate_words = (w_zi_words, w_zl_words, w_zt_words, w_zd_words)
    gate_scales = (w_zi_scales, w_zl_scales, w_zt_scales, w_zd_scales)
    gate_bias = (b_zi, b_zl, b_zt, b_zd)
    q_parts = (left_state, top_state, diagonal_state, x)

    def by_partition(rows):
        return rows.rearrange("(p t) c -> p t c", t=ROWS_PER_PARTITION)

    with ExitStack() as ctx:
        ctx.enter_context(tc.manual_schedule())
        keep = ctx.enter_context(tc.tile_pool(name="keep", bufs=1))
        rows_pool = ctx.enter_context(tc.tile_pool(name="rows", bufs=LOAD_AHEAD + 1))
        grouped_pool = ctx.enter_context(tc.tile_pool(name="grouped", bufs=2))
        pairs = ctx.enter_context(tc.tile_pool(name="pairs", bufs=2))
        triples = ctx.enter_context(tc.tile_pool(name="triples", bufs=3))
        fours = ctx.enter_context(tc.tile_pool(name="fours", bufs=4))
        waiting = ctx.enter_context(tc.tile_pool(name="waiting", bufs=BATCH + 2))
        gate_psum = ctx.enter_context(tc.psum_pool(name="gate_psum", bufs=1))
        state_psum = ctx.enter_context(tc.psum_pool(name="state_psum", bufs=1))
        blend_psum = ctx.enter_context(tc.psum_pool(name="blend_psum", bufs=1))
        turn_psum = ctx.enter_context(tc.psum_pool(name="turn_psum", bufs=2))

        w_codes = keep.tile([P, GATES, PASSES, UNITS], U32, align_bytes=64)
        w_planes = keep.tile([P, GATES, PASSES, UNITS], U8, align_bytes=64)
        bias_rows = keep.tile([P, P], BF16)
        bias = keep.tile([P, GATES * HALVES], F32)
        ident_bf16 = keep.tile([P, P], BF16)
        ident_f32 = keep.tile([P, P], F32)

        nc.vector.memset(w_planes[:].bitcast(I32), 0)
        nc.vector.memset(bias_rows[:].bitcast(I32), 0)
        make_identity(nc, ident_f32[:])
        make_identity(nc, ident_bf16[:])

        q_rows = {}
        h_rows = {}

        def load_rows(b):
            tiles = slice(b * TILES, (b + 1) * TILES)
            q_rows[b] = rows_pool.tile([P, TILES, K], BF16, name="q_rows")
            h_rows[b] = rows_pool.tile([P, TILES, UNITS], BF16, name="h_rows")
            for part, rows in enumerate(q_parts):
                nc.sync.dma_start(
                    out=q_rows[b][:, :, part * UNITS : (part + 1) * UNITS],
                    in_=by_partition(rows)[:, tiles, :],
                )

        def load_candidate(b):
            tiles = slice(b * TILES, (b + 1) * TILES)
            nc.sync.dma_start(out=h_rows[b][:], in_=by_partition(h_cand)[:, tiles, :])

        load_rows(0)
        for j in range(GATES):
            nc.sync.dma_start(
                out=w_codes[:, j, :, :].bitcast(I32),
                in_=gate_words[j].rearrange("g p n t -> p g (n t)").bitcast(I32),
            )
        for j in range(GATES):
            scale_rows = gate_scales[j].rearrange("g q n -> q g n")
            for quadrant in range(4):
                nc.sync.dma_start(
                    out=w_planes[32 * quadrant : 32 * quadrant + 4, j, :, :].bitcast(I32),
                    in_=scale_rows[4 * quadrant : 4 * quadrant + 4, :, :].bitcast(I32),
                )
            nc.scalar.dma_start(
                out=bias_rows[HALVES * j : HALVES * (j + 1), :],
                in_=gate_bias[j].rearrange("(h u) -> h u", h=HALVES),
            )
        load_candidate(0)
        for b in range(1, LOAD_AHEAD):
            load_rows(b)
            load_candidate(b)

        def bias_of(s, j):
            column = HALVES * j + s % HALVES
            return bias[:, column : column + 1]

        grouped = {}
        turned = {}
        states_t = {}
        q_codes = {}
        q_planes = {}
        acc = {}
        states_v = {}
        states_g = {}
        top_gate = {}
        weights = {}
        products = {}
        halves = {}
        total_rows = {}
        total = {}
        log_rows = {}
        blend = {}
        out_rows = {}

        def turn_q(c, pair):
            b, g = divmod(c, PASSES)
            turned[c, pair] = turn_psum.tile([P, 2, 2 * P], F32, name="turned", tag="turn")
            for i in range(2):
                words = q_rows[b][:, 2 * pair + i, :].bitcast(F32)
                for u in range(2):
                    nc.tensor.transpose(
                        turned[c, pair][:, u, i * P : (i + 1) * P],
                        words[:, WORDS * g + u : WORDS * (g + 1) : 2],
                        ident_f32[:],
                    )

        def group_q(c, pair):
            b, g = divmod(c, PASSES)
            if g == 0 and pair == 0:
                grouped[b] = grouped_pool.tile([P, PASSES, 4 * COLS], BF16, name="grouped", align_bytes=64)
            side_by_side = grouped[b][:, g, pair * 8 * P : (pair + 1) * 8 * P].bitcast(F32)
            nc.scalar.copy(
                out=side_by_side.rearrange("p (c u) -> p c u", u=2),
                in_=turned[c, pair][:].rearrange("p u c -> p c u"),
            )

        def transpose_q(c):
            for pair in range(TILES // 2):
                turn_q(c, pair)
                group_q(c, pair)

        def quantise_q(b):
            q_codes[b] = pairs.tile([P, PASSES, COLS], U32, name="q_codes", align_bytes=64)
            q_planes[b] = pairs.tile([P, PASSES, COLS], U8, name="q_planes", align_bytes=64)
            nc.vector.quantize_mx(
                out=q_codes[b][:].rearrange("p g c -> p (g c)").bitcast(FP8X4),
                scales=q_planes[b][:].rearrange("p g c -> p (g c)"),
                in_=grouped[b][:].rearrange("p g c -> p (g c)"),
            )

        def multiply(s, j):
            b, h = divmod(s, HALVES)
            units = slice(h * P, (h + 1) * P)
            acc[s, j] = gate_psum.tile([P, COLS], F32, name="acc%d" % j)
            for g in range(PASSES):
                nc.tensor.matmul_mx(
                    out=acc[s, j][:],
                    lhsT=w_codes[:, j, g, units].bitcast(FP8X4),
                    lhsT_scale=w_planes[:, j, g, units],
                    rhs=q_codes[b][:, g, :].bitcast(FP8X4),
                    rhs_scale=q_planes[b][:, g, :],
                    start=(g == 0),
                    stop=(g == PASSES - 1),
                )

        def first_gate(s):
            top_gate[s] = pairs.tile([P, COLS], F32, name="top_gate")
            nc.scalar.activation(
                out=top_gate[s][:], in_=acc[s, 0][:], func=ACT.Identity, bias=bias_of(s, 0), scale=1.0
            )

        def larger_gate(s, j):
            nc.vector.scalar_tensor_tensor(
                out=top_gate[s][:], in0=acc[s, j][:], scalar=bias_of(s, j), in1=top_gate[s][:],
                op0=ALU.add, op1=ALU.max,
            )

        def below_top(s, j):
            if j == 0:
                weights[s] = fours.tile([P, GATES, COLS], F32, name="weights")
            nc.vector.scalar_tensor_tensor(
                out=weights[s][:, j, :], in0=acc[s, j][:], scalar=bias_of(s, j), in1=top_gate[s][:],
                op0=ALU.add, op1=ALU.subtract,
            )

        def exponentials(s, pair):
            two_gates = weights[s][:, 2 * pair : 2 * pair + 2, :]
            nc.scalar.activation(out=two_gates, in_=two_gates, func=ACT.Exp)

        def state_rows(s, j, t):
            b, h = divmod(s, HALVES)
            if j == 0:
                return h_rows[b][:, t, h * P : (h + 1) * P]
            first = (j - 1) * UNITS + h * P
            return q_rows[b][:, t, first : first + P]

        spare_banks = [0]

        def spare(shape, dtype):
            spare_banks[0] += 1
            return gate_psum.tile(shape, dtype, name="acc%d" % (spare_banks[0] % GATES))

        def transpose_states(s, pair, bank):
            for j in range(2):
                for t in range(TILES):
                    nc.tensor.transpose(bank[:, j, t * P : (t + 1) * P], state_rows(s, 2 * pair + j, t), ident_bf16[:])
            states_t[s, pair] = bank

        def transpose_states_v(s):
            transpose_states(s, 0, state_psum.tile([P, 2, COLS], BF16, name="states_v"))

        def transpose_states_g(s):
            transpose_states(s, 1, turn_psum.tile([P, 2, COLS], BF16, name="states_t", tag="turn"))

        def copy_state_l(s):
            states_g[s] = fours.tile([P, 3, COLS], BF16, name="states_g")
            nc.scalar.copy(out=states_g[s][:, 0, :], in_=states_t[s, 0][:, 1, :])

        def copy_states_g(s):
            nc.scalar.copy(out=states_g[s][:, 1:3, :], in_=states_t[s, 1][:])

        def weigh_first(s):
            nc.vector.tensor_tensor(
                out=products[s][:, 0, :], in0=weights[s][:, 0, :], in1=states_t[s, 0][:, 0, :], op=ALU.mult
            )

        def open_products(s):
            products[s] = waiting.tile([P, GATES, COLS], F32, name="products")

        def weigh_v(s, pair=0):
            two_gates = slice(2 * pair, 2 * pair + 2)
            nc.vector.tensor_tensor(
                out=products[s][:, two_gates, :], in0=weights[s][:, two_gates, :], in1=states_t[s, pair][:], op=ALU.mult
            )

        def weigh_g(s):
            nc.gpsimd.tensor_tensor(
                out=products[s][:, 1:4, :], in0=weights[s][:, 1:4, :], in1=states_g[s][:], op=ALU.mult
            )

        def add_pairs(s, engine):
            halves[s] = pairs.tile([P, 2, COLS], F32, name="halves")
            engine.tensor_tensor(
                out=halves[s][:], in0=weights[s][:, 0:2, :], in1=weights[s][:, 2:4, :], op=ALU.add
            )

        def add_halves(s, engine):
            total[s] = waiting.tile([P, COLS], F32, name="total")
            engine.tensor_tensor(out=total[s][:], in0=halves[s][:, 0, :], in1=halves[s][:, 1, :], op=ALU.add)

        def logarithm(s):
            nc.scalar.activation(out=total[s][:], in_=total[s][:], func=ACT.Ln)

        def turn_log(s):
            log_rows[s] = turn_psum.tile([P, COLS], F32, name="log_t", tag="turn")
            for t in range(TILES):
                nc.tensor.transpose(log_rows[s][:, t * P : (t + 1) * P], total[s][:, t * P : (t + 1) * P], ident_f32[:])

        def invert(s):
            total_rows[s] = fours.tile([P, COLS], F32, name="total_rows")
            nc.scalar.activation(out=total_rows[s][:], in_=log_rows[s][:], func=ACT.Exp, scale=-1.0)

        def sum_products(s, in_spare=False):
            if in_spare:
                blend[s] = spare([P, TILES, P], F32)
            else:
                blend[s] = blend_psum.tile([P, TILES, P], F32, name="blend")
            for t in range(TILES):
                for j in range(GATES):
                    nc.tensor.matmul(
                        out=blend[s][:, t, :], lhsT=products[s][:, j, t * P : (t + 1) * P], rhs=ident_f32[:],
                        is_transpose=True, start=(j == 0), stop=(j == GATES - 1),
                    )

        def normalise(s):
            b, h = divmod(s, HALVES)
            if h == 0:
                out_rows[b] = triples.tile([P, TILES, UNITS], F32, name="out_rows")
            nc.vector.tensor_tensor(
                out=out_rows[b][:, :, h * P : (h + 1) * P], in0=blend[s][:],
                in1=total_rows[s][:].rearrange("p (t u) -> p t u", t=TILES), op=ALU.mult,
            )
            if b == BLOCKS - 1:
                units = slice(h * P, (h + 1) * P)
                nc.sync.dma_start(out=by_partition(out)[:, b * TILES : (b + 1) * TILES, units], in_=out_rows[b][:, :, units])
            elif h == HALVES - 1:
                nc.sync.dma_start(out=by_partition(out)[:, b * TILES : (b + 1) * TILES, :], in_=out_rows[b][:])

        transpose_q(0)
        transpose_q(1)
        quantise_q(0)
        bias_turned = turn_psum.tile([P, P], BF16, tag="turn")
        nc.tensor.transpose(bias_turned[:], bias_rows[:], ident_bf16[:])
        nc.vector.tensor_copy(out=bias[:], in_=bias_turned[:, 0 : GATES * HALVES])
        for j in range(GATES):
            multiply(0, j)
        first_gate(0)
        transpose_q(2)
        transpose_q(3)
        for j in range(1, GATES):
            larger_gate(0, j)

        def live(s):
            return 0 <= s < STAGES

        LAG = BATCH + 1
        last = STAGES - 1
        for s in range(STAGES):
            a = s - LAG
            burst = s % BATCH == 0 and live(s - 1)
            after = s % BATCH == 1 and live(s - 2)
            quantising = s % 2 == 0 and s // 2 + 1 < BLOCKS
            c = s + TURN_AHEAD
            if live(a) and not after:
                invert(a)
            if s == last:
                turn_log(a + 1)
                invert(a + 1)
            for j in range(GATES):
                below_top(s, j)
                if live(s + 1):
                    multiply(s + 1, j)
                if j == 0 and live(s + 1):
                    first_gate(s + 1)
                if j == 0 and after:
                    logarithm(s - 3)
                    logarithm(s - 2)
                    invert(a)
                if j % 2 == 1:
                    exponentials(s, j // 2)
            if live(a - 1):
                normalise(a - 1)
            if live(s - 1) and s < last:
                open_products(s - 1)
                weigh_first(s - 1)
                weigh_g(s - 1)
            if quantising:
                quantise_q(s // 2 + 1)
            if live(s + 1):
                larger_gate(s + 1, 1)
                larger_gate(s + 1, 2)
                larger_gate(s + 1, 3)
            if c < CHUNKS:
                turn_q(c, 0)
                group_q(c, 0)
            if burst:
                logarithm(s - 4)
            if live(a):
                sum_products(a)
            if c < CHUNKS:
                turn_q(c, 1)
                group_q(c, 1)
            if burst:
                logarithm(s - 3)
            if s < last:
                transpose_states_v(s)
                add_pairs(s, nc.gpsimd)
                add_halves(s, nc.gpsimd)
            if s < last - 1:
                copy_state_l(s)
                transpose_states_g(s)
                copy_states_g(s)
            if s < last and live(a + 1):
                turn_log(a + 1)
            if s % HALVES == 1 and s // HALVES + LOAD_AHEAD < BLOCKS:
                load_rows(s // HALVES + LOAD_AHEAD)
                load_candidate(s // HALVES + LOAD_AHEAD)

        summed = last - LAG
        batch = list(range(STAGES - BATCH, STAGES))
        add_pairs(last, nc.vector)
        add_halves(last, nc.vector)
        for s in batch:
            logarithm(s)
        transpose_states(last - 1, 1, spare([P, 2, COLS], BF16))
        transpose_states(last, 0, spare([P, 2, COLS], BF16))
        transpose_states(last, 1, spare([P, 2, COLS], BF16))
        normalise(summed)
        turn_log(batch[0])
        turn_log(batch[1])
        sum_products(summed + 1)
        sum_products(batch[0], in_spare=True)
        for s in (last - 1, last):
            open_products(s)
            weigh_v(s, 0)
            weigh_v(s, 1)
        normalise(summed + 1)
        sum_products(batch[1], in_spare=True)
        invert(batch[0])
        invert(batch[1])
        turn_log(batch[2])
        turn_log(batch[3])
        sum_products(batch[2], in_spare=True)
        sum_products(batch[3], in_spare=True)
        invert(batch[2])
        invert(batch[3])
        for s in batch:
            normalise(s)
